import numpy as np
import ml_dtypes


def mxq(x, axis, fmt="e4m3"):
    dtype, down = {"e4m3": (ml_dtypes.float8_e4m3fn, 7), "e5m2": (ml_dtypes.float8_e5m2, 14)}[fmt]
    v = np.moveaxis(np.asarray(x, np.float32).astype(ml_dtypes.bfloat16).astype(np.float64), axis, -1)
    blocks = v.reshape(v.shape[:-1] + (-1, 32))
    amax = np.abs(blocks).max(-1, keepdims=True)
    byte = np.maximum(np.where(amax > 0, np.frexp(amax)[1] - 1 + 127, 0) - down, 1)
    scale = np.exp2(byte - 127.0)
    codes = (blocks / scale).astype(np.float32).astype(dtype).astype(np.float64)
    return np.moveaxis((codes * scale).reshape(v.shape), -1, axis)


WIDE = False


def mx_kscale(k):
    if not WIDE:
        return np.ones(k)
    levels = np.array([10, -10, 5, -5, 0])
    if k % 512:
        return np.exp2(np.random.permutation(np.resize(levels, k // 32))).repeat(32)
    a = np.empty((k // 512, 16))
    for p in range(k // 512):
        a[p, :8] = np.random.permutation(np.resize(levels, 8))
        for g in range(8):
            far = levels[np.abs(levels - a[p, g]) >= 10]
            a[p, g + 8] = far[np.random.randint(len(far))]
    return np.exp2(a.ravel()).repeat(32)


BF16 = ml_dtypes.bfloat16


def bf(x):
    return np.asarray(x, np.float32).astype(BF16)


def f64(x):
    return np.asarray(x).astype(np.float64)


B, DIN, H1, H2, N, I, K, O = 8192, 2048, 1024, 512, 32, 16, 128, 8
KO = K * O
SQ_EPS = 1e-8


def squash(t):
    sq = np.sum(t * t, axis=-1, keepdims=True)
    return (sq / (1.0 + sq)) * t / np.sqrt(sq + SQ_EPS)


def setup_inputs():
    amp = np.exp(0.8 * np.random.standard_normal((B, K, 1)))
    t = np.repeat(np.asarray(mx_kscale(KO))[::O], O)
    h = np.exp2(np.round(np.log2(t) / 2))
    c = h / h.max()
    d = np.where(c < 1.0, 0.0625, 1.0)
    return {"s": bf(np.random.standard_normal((B, K, O)) * amp * 1.4 / np.sqrt(O) * c.reshape(K, O)),
            "Wc": bf(np.random.standard_normal((KO, K)) * 6.0 / np.sqrt(KO) * (d / (c * c))[:, None]),
            "bc": bf(np.random.standard_normal(K) * 0.2)}


def reference(s, Wc, bc):
    v = squash(f64(s)).reshape(B, KO)
    return (mxq(v, 1, "e4m3") @ mxq(f64(Wc), 0, "e4m3")) + f64(bc)

@@ -1,0 +1,247 @@
+from contextlib import ExitStack
+
+import concourse.mybir as mybir
+from concourse.masks import make_identity
+
+F32 = mybir.dt.float32
+BF16 = mybir.dt.bfloat16
+U32 = mybir.dt.uint32
+U8 = mybir.dt.uint8
+FP8X4 = mybir.dt.float8_e4m3fn_x4
+ALU = mybir.AluOpType
+ACT = mybir.ActivationFunctionType
+
+P = 128
+ROWS = 8192
+CAPS = 128
+CAP_LEN = 8
+HALF_CAP = CAP_LEN // 2
+K = CAPS * CAP_LEN
+N_OUT = 128
+SQ_EPS = 1e-8
+
+SUB = 2
+GROUPS = ROWS // (P * SUB)
+TILES = GROUPS * SUB
+PASSES = K // (4 * P)
+HALVES = 2
+
+LOADS_AHEAD = 8
+LAG_SUMS = 3
+LAG_ONE_PLUS = LAG_SUMS + 1
+LAG_DENOM = LAG_ONE_PLUS + 1
+LAG_RECIP = LAG_DENOM + 1
+LAG_FACTOR = LAG_RECIP + 1
+LAG_SCALE = LAG_FACTOR + SUB
+LAG_TRANSPOSE = LAG_SCALE + 1
+LAG_EVACUATE = LAG_TRANSPOSE + 1
+LAG_QUANTISE = LAG_EVACUATE + 1
+LAG_MULTIPLY = LAG_QUANTISE + 1
+LAG_FINISH = LAG_MULTIPLY + 1
+
+FLOPS = 2 * ROWS * K * N_OUT
+
+
+def tile_capsulenetwork_pc_t_kernel(tc, s, Wc, bc, out):
+    nc = tc.nc
+    with ExitStack() as ctx:
+        const = ctx.enter_context(tc.tile_pool(name="const", bufs=1))
+        x_pool = ctx.enter_context(tc.tile_pool(name="x", bufs=LOADS_AHEAD + LAG_SCALE + 3))
+        sq_pool = ctx.enter_context(tc.tile_pool(name="sq", bufs=3))
+        hs_pool = ctx.enter_context(tc.tile_pool(name="hs", bufs=LAG_SUMS + 2))
+        small = ctx.enter_context(tc.tile_pool(name="small", bufs=2))
+        v_pool = ctx.enter_context(tc.tile_pool(name="v", bufs=4))
+        mx_pool = ctx.enter_context(tc.tile_pool(name="mx", bufs=2))
+        res_pool = ctx.enter_context(tc.tile_pool(name="res", bufs=2))
+        q_psum = ctx.enter_context(tc.psum_pool(name="q_psum", bufs=3))
+        f_psum = ctx.enter_context(tc.psum_pool(name="f_psum", bufs=2))
+        t_psum = ctx.enter_context(tc.psum_pool(name="t_psum", bufs=2))
+        o_psum = ctx.enter_context(tc.psum_pool(name="o_psum", bufs=1))
+
+        s_tiles = s.rearrange("(g p r) j o -> g r p (j o)", p=P, r=SUB)
+        out_groups = out.rearrange("(g p r) n -> g p (r n)", p=P, r=SUB)
+
+        x_of = {}
+        hs_of = {}
+        q_of = {}
+        one_plus_of = {}
+        denom_of = {}
+        recip_of = {}
+        f_of = {}
+        v_of = {}
+        vt_of = {}
+        grouped_of = {}
+        codes_of = {}
+        scales_of = {}
+        acc_of = {}
+
+        def load(t):
+            x = x_pool.tile([P, CAPS, CAP_LEN], BF16)
+            nc.sync.dma_start(out=x[:].rearrange("p j o -> p (j o)"), in_=s_tiles[t // SUB, t % SUB])
+            x_of[t] = x
+
+        def squares(t):
+            sq = sq_pool.tile([P, CAPS, CAP_LEN], F32)
+            nc.scalar.activation(out=sq[:], in_=x_of[t][:], func=ACT.Square)
+            hs = hs_pool.tile([P, CAPS, HALF_CAP], F32)
+            nc.gpsimd.tensor_tensor(
+                out=hs[:], in0=sq[:, :, 0:HALF_CAP], in1=sq[:, :, HALF_CAP:CAP_LEN], op=ALU.add
+            )
+            hs_of[t] = hs
+
+        def sums(t):
+            if t % SUB == 0:
+                q_t = q_psum.tile([P, SUB, P], F32)
+                q_of[t // SUB] = q_t
+            for d in range(HALF_CAP):
+                nc.tensor.matmul(
+                    out=q_of[t // SUB][:, t % SUB, :],
+                    lhsT=hs_of[t][:, :, d],
+                    rhs=ident[:],
+                    is_transpose=True,
+                    start=(d == 0),
+                    stop=(d == HALF_CAP - 1),
+                )
+
+        def one_plus(g):
+            one_plus_sq = small.tile([P, SUB, P], F32)
+            nc.scalar.activation(out=one_plus_sq[:], in_=q_of[g][:], func=ACT.Square, bias=one_col[:, 0:1])
+            one_plus_of[g] = one_plus_sq
+
+        def denom(g):
+            denom_sq = small.tile([P, SUB, P], F32)
+            nc.vector.scalar_tensor_tensor(
+                out=denom_sq[:], in0=q_of[g][:], scalar=SQ_EPS, in1=one_plus_of[g][:], op0=ALU.add, op1=ALU.mult
+            )
+            denom_of[g] = denom_sq
+
+        def recip(g):
+            recip_t = small.tile([P, SUB, P], F32)
+            nc.scalar.activation(out=recip_t[:], in_=denom_of[g][:], func=ACT.Abs_reciprocal_sqrt)
+            recip_of[g] = recip_t
+
+        def factor(g):
+            f_t = small.tile([P, SUB, P], F32)
+            nc.vector.tensor_tensor(out=f_t[:], in0=q_of[g][:], in1=recip_of[g][:], op=ALU.mult)
+            f_rows = f_psum.tile([P, SUB, CAPS], F32)
+            for r in range(SUB):
+                nc.tensor.transpose(out=f_rows[:, r, :], in_=f_t[:, r, :], identity=ident[:])
+            f_of[g] = f_rows
+
+        def scale(t):
+            v = v_pool.tile([P, HALVES, CAPS, HALVES, 2], BF16)
+            for u in range(HALVES):
+                nc.vector.tensor_tensor(
+                    out=v[:, u],
+                    in0=x_of[t][:].rearrange("p j (h u e) -> p u j h e", h=2, u=2)[:, u],
+                    in1=f_of[t // SUB][:, t % SUB, :].unsqueeze(2).unsqueeze(3).to_broadcast([P, CAPS, 2, 2]),
+                    op=ALU.mult,
+                )
+            v_of[t] = v
+
+        def transpose(t):
+            v_words = v_of[t][:].rearrange("p u j h e -> p (u j h e)").bitcast(F32)
+            v_t = t_psum.tile([P, PASSES, HALVES, P], F32)
+            for c in range(PASSES):
+                for u in range(HALVES):
+                    first = (u * PASSES + c) * P
+                    nc.tensor.transpose(
+                        out=v_t[:, c, u, :], in_=v_words[:, first : first + P], identity=ident[:]
+                    )
+            vt_of[t] = v_t
+
+        def evacuate(t):
+            if t % SUB == 0:
+                grouped = mx_pool.tile([P, SUB, PASSES, P, HALVES], F32, align_bytes=64)
+                grouped_of[t // SUB] = grouped
+            nc.scalar.copy(
+                out=grouped_of[t // SUB][:, t % SUB], in_=vt_of[t][:].rearrange("q c u p -> q c p u")
+            )
+
+        def quantise(g):
+            codes = mx_pool.tile([P, SUB, PASSES, P], U32, align_bytes=64)
+            scales = mx_pool.tile([P, SUB, PASSES, P], U8, align_bytes=64)
+            nc.vector.quantize_mx(
+                out=codes[:].rearrange("q r c p -> q (r c p)").bitcast(FP8X4),
+                scales=scales[:].rearrange("q r c p -> q (r c p)"),
+                in_=grouped_of[g][:].rearrange("q r c p u -> q (r c p u)").bitcast(BF16),
+            )
+            codes_of[g] = codes
+            scales_of[g] = scales
+
+        def multiply(g):
+            acc = o_psum.tile([P, SUB, N_OUT], F32)
+            for r in range(SUB):
+                for c in range(PASSES):
+                    nc.tensor.matmul_mx(
+                        out=acc[:, r, :],
+                        lhsT=codes_of[g][:, r, c, :].bitcast(FP8X4),
+                        lhsT_scale=scales_of[g][:, r, c, :],
+                        rhs=w_codes[:, c, :].bitcast(FP8X4),
+                        rhs_scale=w_scales[:, c, :],
+                        start=(c == 0),
+                        stop=(c == PASSES - 1),
+                    )
+            acc_of[g] = acc
+
+        def finish(g):
+            res = res_pool.tile([P, SUB, N_OUT], F32)
+            nc.vector.tensor_tensor(
+                out=res[:],
+                in0=acc_of[g][:],
+                in1=bias[:].unsqueeze(1).to_broadcast([P, SUB, N_OUT]),
+                op=ALU.add,
+            )
+            nc.sync.dma_start(out=out_groups[g], in_=res[:].rearrange("p r n -> p (r n)"))
+
+        def for_tile(stage, t):
+            if 0 <= t < TILES:
+                stage(t)
+
+        def for_group(stage, t):
+            if 0 <= t < TILES and t % SUB == SUB - 1:
+                stage(t // SUB)
+
+        with tc.manual_schedule():
+            for t in range(LOADS_AHEAD):
+                load(t)
+
+            ident = const.tile([P, P], F32)
+            make_identity(nc, ident[:])
+            one_col = const.tile([P, 1], F32)
+            nc.vector.memset(one_col[:], 1.0)
+
+            bias_bf = const.tile([P, N_OUT], BF16)
+            nc.sync.dma_start(out=bias_bf[:], in_=bc.partition_broadcast(P))
+            bias = const.tile([P, N_OUT], F32)
+            nc.vector.tensor_copy(out=bias[:], in_=bias_bf[:])
+
+            w_raw = const.tile([P, PASSES, 2 * HALVES, N_OUT], BF16)
+            nc.sync.dma_start(
+                out=w_raw[:].rearrange("q c t n -> q c (t n)"),
+                in_=Wc.rearrange("(c q t) n -> q c (t n)", q=P, t=2 * HALVES),
+            )
+            w_grouped = const.tile([P, PASSES, N_OUT, 2 * HALVES], BF16, align_bytes=64)
+            nc.vector.tensor_copy(out=w_grouped[:], in_=w_raw[:].rearrange("q c t n -> q c n t"))
+            w_codes = const.tile([P, PASSES, N_OUT], U32, align_bytes=64)
+            w_scales = const.tile([P, PASSES, N_OUT], U8, align_bytes=64)
+            nc.vector.quantize_mx(
+                out=w_codes[:].rearrange("q c n -> q (c n)").bitcast(FP8X4),
+                scales=w_scales[:].rearrange("q c n -> q (c n)"),
+                in_=w_grouped[:].rearrange("q c n t -> q (c n t)"),
+            )
+
+            for step in range(TILES + LAG_FINISH):
+                for_tile(sums, step - LAG_SUMS)
+                for_group(factor, step - LAG_FACTOR)
+                for_group(denom, step - LAG_DENOM)
+                for_tile(scale, step - LAG_SCALE)
+                for_tile(transpose, step - LAG_TRANSPOSE)
+                for_tile(evacuate, step - LAG_EVACUATE)
+                for_group(quantise, step - LAG_QUANTISE)
+                for_group(multiply, step - LAG_MULTIPLY)
+                for_group(finish, step - LAG_FINISH)
+                for_group(recip, step - LAG_RECIP)
+                for_group(one_plus, step - LAG_ONE_PLUS)
+                for_tile(squares, step)
+                for_tile(load, step + LOADS_AHEAD)

@@ -15,7 +15,6 @@ P = 128
 ROWS = 8192
 CAPS = 128
 CAP_LEN = 8
-HALF_CAP = CAP_LEN // 2
 K = CAPS * CAP_LEN
 N_OUT = 128
 SQ_EPS = 1e-8
@@ -27,7 +26,7 @@ PASSES = K // (4 * P)
 HALVES = 2
 
 LOADS_AHEAD = 8
-LAG_SUMS = 3
+LAG_SUMS = 2
 LAG_ONE_PLUS = LAG_SUMS + 1
 LAG_DENOM = LAG_ONE_PLUS + 1
 LAG_RECIP = LAG_DENOM + 1
@@ -47,8 +46,7 @@ def tile_capsulenetwork_pc_t_kernel(tc, s, Wc, bc, out):
     with ExitStack() as ctx:
         const = ctx.enter_context(tc.tile_pool(name="const", bufs=1))
         x_pool = ctx.enter_context(tc.tile_pool(name="x", bufs=LOADS_AHEAD + LAG_SCALE + 3))
-        sq_pool = ctx.enter_context(tc.tile_pool(name="sq", bufs=3))
-        hs_pool = ctx.enter_context(tc.tile_pool(name="hs", bufs=LAG_SUMS + 2))
+        sq_pool = ctx.enter_context(tc.tile_pool(name="sq", bufs=LAG_SUMS + 2))
         small = ctx.enter_context(tc.tile_pool(name="small", bufs=2))
         v_pool = ctx.enter_context(tc.tile_pool(name="v", bufs=4))
         mx_pool = ctx.enter_context(tc.tile_pool(name="mx", bufs=2))
@@ -62,7 +60,7 @@ def tile_capsulenetwork_pc_t_kernel(tc, s, Wc, bc, out):
         out_groups = out.rearrange("(g p r) n -> g p (r n)", p=P, r=SUB)
 
         x_of = {}
-        hs_of = {}
+        sq_of = {}
         q_of = {}
         one_plus_of = {}
         denom_of = {}
@@ -83,24 +81,20 @@ def tile_capsulenetwork_pc_t_kernel(tc, s, Wc, bc, out):
         def squares(t):
             sq = sq_pool.tile([P, CAPS, CAP_LEN], F32)
             nc.scalar.activation(out=sq[:], in_=x_of[t][:], func=ACT.Square)
-            hs = hs_pool.tile([P, CAPS, HALF_CAP], F32)
-            nc.gpsimd.tensor_tensor(
-                out=hs[:], in0=sq[:, :, 0:HALF_CAP], in1=sq[:, :, HALF_CAP:CAP_LEN], op=ALU.add
-            )
-            hs_of[t] = hs
+            sq_of[t] = sq
 
         def sums(t):
             if t % SUB == 0:
                 q_t = q_psum.tile([P, SUB, P], F32)
                 q_of[t // SUB] = q_t
-            for d in range(HALF_CAP):
+            for d in range(CAP_LEN):
                 nc.tensor.matmul(
                     out=q_of[t // SUB][:, t % SUB, :],
-                    lhsT=hs_of[t][:, :, d],
+                    lhsT=sq_of[t][:, :, d],
                     rhs=ident[:],
                     is_transpose=True,
                     start=(d == 0),
-                    stop=(d == HALF_CAP - 1),
+                    stop=(d == CAP_LEN - 1),
                 )
 
         def one_plus(g):

@@ -15,28 +15,21 @@ P = 128
 ROWS = 8192
 CAPS = 128
 CAP_LEN = 8
+HALF_CAP = CAP_LEN // 2
 K = CAPS * CAP_LEN
 N_OUT = 128
 SQ_EPS = 1e-8
-
-SUB = 2
-GROUPS = ROWS // (P * SUB)
-TILES = GROUPS * SUB
+TILES = ROWS // P
 PASSES = K // (4 * P)
 HALVES = 2
 
-LOADS_AHEAD = 8
-LAG_SUMS = 2
-LAG_ONE_PLUS = LAG_SUMS + 1
-LAG_DENOM = LAG_ONE_PLUS + 1
-LAG_RECIP = LAG_DENOM + 1
-LAG_FACTOR = LAG_RECIP + 1
-LAG_SCALE = LAG_FACTOR + SUB
-LAG_TRANSPOSE = LAG_SCALE + 1
-LAG_EVACUATE = LAG_TRANSPOSE + 1
-LAG_QUANTISE = LAG_EVACUATE + 1
-LAG_MULTIPLY = LAG_QUANTISE + 1
-LAG_FINISH = LAG_MULTIPLY + 1
+MAX_GROUP = 4
+ENDS = [1, 1, 2]
+GROUPS = ENDS + [MAX_GROUP] * ((TILES - 2 * sum(ENDS)) // MAX_GROUP) + ENDS[::-1]
+FIRST = [sum(GROUPS[:g]) for g in range(len(GROUPS))]
+GROUP_OF = [g for g, n in enumerate(GROUPS) for r in range(n)]
+VECTOR_SQUARES = (1, 3)
+LOADS_AHEAD = 3
 
 FLOPS = 2 * ROWS * K * N_OUT
 
@@ -45,22 +38,21 @@ def tile_capsulenetwork_pc_t_kernel(tc, s, Wc, bc, out):
     nc = tc.nc
     with ExitStack() as ctx:
         const = ctx.enter_context(tc.tile_pool(name="const", bufs=1))
-        x_pool = ctx.enter_context(tc.tile_pool(name="x", bufs=LOADS_AHEAD + LAG_SCALE + 3))
-        sq_pool = ctx.enter_context(tc.tile_pool(name="sq", bufs=LAG_SUMS + 2))
+        x_pool = ctx.enter_context(tc.tile_pool(name="x", bufs=7))
+        sq_pool = ctx.enter_context(tc.tile_pool(name="sq", bufs=4))
+        hs_pool = ctx.enter_context(tc.tile_pool(name="hs", bufs=4))
         small = ctx.enter_context(tc.tile_pool(name="small", bufs=2))
         v_pool = ctx.enter_context(tc.tile_pool(name="v", bufs=4))
-        mx_pool = ctx.enter_context(tc.tile_pool(name="mx", bufs=2))
+        mx_pool = ctx.enter_context(tc.tile_pool(name="mx", bufs=3))
         res_pool = ctx.enter_context(tc.tile_pool(name="res", bufs=2))
-        q_psum = ctx.enter_context(tc.psum_pool(name="q_psum", bufs=3))
+        q_psum = ctx.enter_context(tc.psum_pool(name="q_psum", bufs=2))
         f_psum = ctx.enter_context(tc.psum_pool(name="f_psum", bufs=2))
-        t_psum = ctx.enter_context(tc.psum_pool(name="t_psum", bufs=2))
+        t_psum = ctx.enter_context(tc.psum_pool(name="t_psum", bufs=3))
         o_psum = ctx.enter_context(tc.psum_pool(name="o_psum", bufs=1))
-
-        s_tiles = s.rearrange("(g p r) j o -> g r p (j o)", p=P, r=SUB)
-        out_groups = out.rearrange("(g p r) n -> g p (r n)", p=P, r=SUB)
 
         x_of = {}
         sq_of = {}
+        hs_of = {}
         q_of = {}
         one_plus_of = {}
         denom_of = {}
@@ -73,62 +65,87 @@ def tile_capsulenetwork_pc_t_kernel(tc, s, Wc, bc, out):
         scales_of = {}
         acc_of = {}
 
-        def load(t):
-            x = x_pool.tile([P, CAPS, CAP_LEN], BF16)
-            nc.sync.dma_start(out=x[:].rearrange("p j o -> p (j o)"), in_=s_tiles[t // SUB, t % SUB])
-            x_of[t] = x
+        def rows_of(g):
+            return slice(FIRST[g] * P, (FIRST[g] + GROUPS[g]) * P)
+
+        def place(t):
+            return GROUP_OF[t], t - FIRST[GROUP_OF[t]]
+
+        def load(g):
+            x = x_pool.tile([P, GROUPS[g], CAPS, CAP_LEN], BF16)
+            nc.sync.dma_start(
+                out=x[:].rearrange("p r j o -> p (r j o)"),
+                in_=s[rows_of(g)].rearrange("(p r) j o -> p (r j o)", r=GROUPS[g]),
+            )
+            x_of[g] = x
 
         def squares(t):
+            g, r = place(t)
             sq = sq_pool.tile([P, CAPS, CAP_LEN], F32)
-            nc.scalar.activation(out=sq[:], in_=x_of[t][:], func=ACT.Square)
+            if t in VECTOR_SQUARES:
+                nc.vector.tensor_tensor(out=sq[:], in0=x_of[g][:, r], in1=x_of[g][:, r], op=ALU.mult)
+            else:
+                nc.scalar.activation(out=sq[:], in_=x_of[g][:, r], func=ACT.Square)
             sq_of[t] = sq
 
+        def halve(t):
+            hs = hs_pool.tile([P, CAPS, HALF_CAP], F32)
+            nc.gpsimd.tensor_tensor(
+                out=hs[:],
+                in0=sq_of[t][:, :, 0:HALF_CAP],
+                in1=sq_of[t][:, :, HALF_CAP:CAP_LEN],
+                op=ALU.add,
+            )
+            hs_of[t] = hs
+
         def sums(t):
-            if t % SUB == 0:
-                q_t = q_psum.tile([P, SUB, P], F32)
-                q_of[t // SUB] = q_t
-            for d in range(CAP_LEN):
+            g, r = place(t)
+            if r == 0:
+                q_t = q_psum.tile([P, GROUPS[g], P], F32)
+                q_of[g] = q_t
+            for d in range(HALF_CAP):
                 nc.tensor.matmul(
-                    out=q_of[t // SUB][:, t % SUB, :],
-                    lhsT=sq_of[t][:, :, d],
+                    out=q_of[g][:, r, :],
+                    lhsT=hs_of[t][:, :, d],
                     rhs=ident[:],
                     is_transpose=True,
                     start=(d == 0),
-                    stop=(d == CAP_LEN - 1),
+                    stop=(d == HALF_CAP - 1),
                 )
 
         def one_plus(g):
-            one_plus_sq = small.tile([P, SUB, P], F32)
+            one_plus_sq = small.tile([P, GROUPS[g], P], F32)
             nc.scalar.activation(out=one_plus_sq[:], in_=q_of[g][:], func=ACT.Square, bias=one_col[:, 0:1])
             one_plus_of[g] = one_plus_sq
 
         def denom(g):
-            denom_sq = small.tile([P, SUB, P], F32)
+            denom_sq = small.tile([P, GROUPS[g], P], F32)
             nc.vector.scalar_tensor_tensor(
                 out=denom_sq[:], in0=q_of[g][:], scalar=SQ_EPS, in1=one_plus_of[g][:], op0=ALU.add, op1=ALU.mult
             )
             denom_of[g] = denom_sq
 
         def recip(g):
-            recip_t = small.tile([P, SUB, P], F32)
+            recip_t = small.tile([P, GROUPS[g], P], F32)
             nc.scalar.activation(out=recip_t[:], in_=denom_of[g][:], func=ACT.Abs_reciprocal_sqrt)
             recip_of[g] = recip_t
 
         def factor(g):
-            f_t = small.tile([P, SUB, P], F32)
+            f_t = small.tile([P, GROUPS[g], P], F32)
             nc.vector.tensor_tensor(out=f_t[:], in0=q_of[g][:], in1=recip_of[g][:], op=ALU.mult)
-            f_rows = f_psum.tile([P, SUB, CAPS], F32)
-            for r in range(SUB):
+            f_rows = f_psum.tile([P, GROUPS[g], CAPS], F32)
+            for r in range(GROUPS[g]):
                 nc.tensor.transpose(out=f_rows[:, r, :], in_=f_t[:, r, :], identity=ident[:])
             f_of[g] = f_rows
 
         def scale(t):
-            v = v_pool.tile([P, HALVES, CAPS, HALVES, 2], BF16)
+            g, r = place(t)
+            v = v_pool.tile([P, HALVES, CAPS, 2, 2], BF16)
             for u in range(HALVES):
                 nc.vector.tensor_tensor(
                     out=v[:, u],
-                    in0=x_of[t][:].rearrange("p j (h u e) -> p u j h e", h=2, u=2)[:, u],
-                    in1=f_of[t // SUB][:, t % SUB, :].unsqueeze(2).unsqueeze(3).to_broadcast([P, CAPS, 2, 2]),
+                    in0=x_of[g][:, r].rearrange("p j (h u e) -> p u j h e", h=2, u=HALVES)[:, u],
+                    in1=f_of[g][:, r, :].unsqueeze(2).unsqueeze(3).to_broadcast([P, CAPS, 2, 2]),
                     op=ALU.mult,
                 )
             v_of[t] = v
@@ -145,16 +162,15 @@ def tile_capsulenetwork_pc_t_kernel(tc, s, Wc, bc, out):
             vt_of[t] = v_t
 
         def evacuate(t):
-            if t % SUB == 0:
-                grouped = mx_pool.tile([P, SUB, PASSES, P, HALVES], F32, align_bytes=64)
-                grouped_of[t // SUB] = grouped
-            nc.scalar.copy(
-                out=grouped_of[t // SUB][:, t % SUB], in_=vt_of[t][:].rearrange("q c u p -> q c p u")
-            )
+            g, r = place(t)
+            if r == 0:
+                grouped = mx_pool.tile([P, GROUPS[g], PASSES, P, HALVES], F32, align_bytes=64)
+                grouped_of[g] = grouped
+            nc.scalar.copy(out=grouped_of[g][:, r], in_=vt_of[t][:].rearrange("q c u p -> q c p u"))
 
         def quantise(g):
-            codes = mx_pool.tile([P, SUB, PASSES, P], U32, align_bytes=64)
-            scales = mx_pool.tile([P, SUB, PASSES, P], U8, align_bytes=64)
+            codes = mx_pool.tile([P, GROUPS[g], PASSES, P], U32, align_bytes=64)
+            scales = mx_pool.tile([P, GROUPS[g], PASSES, P], U8, align_bytes=64)
             nc.vector.quantize_mx(
                 out=codes[:].rearrange("q r c p -> q (r c p)").bitcast(FP8X4),
                 scales=scales[:].rearrange("q r c p -> q (r c p)"),
@@ -164,8 +180,8 @@ def tile_capsulenetwork_pc_t_kernel(tc, s, Wc, bc, out):
             scales_of[g] = scales
 
         def multiply(g):
-            acc = o_psum.tile([P, SUB, N_OUT], F32)
-            for r in range(SUB):
+            acc = o_psum.tile([P, GROUPS[g], N_OUT], F32)
+            for r in range(GROUPS[g]):
                 for c in range(PASSES):
                     nc.tensor.matmul_mx(
                         out=acc[:, r, :],
@@ -179,63 +195,84 @@ def tile_capsulenetwork_pc_t_kernel(tc, s, Wc, bc, out):
             acc_of[g] = acc
 
         def finish(g):
-            res = res_pool.tile([P, SUB, N_OUT], F32)
+            res = res_pool.tile([P, GROUPS[g], N_OUT], F32)
             nc.vector.tensor_tensor(
                 out=res[:],
                 in0=acc_of[g][:],
-                in1=bias[:].unsqueeze(1).to_broadcast([P, SUB, N_OUT]),
+                in1=bias[:].unsqueeze(1).to_broadcast([P, GROUPS[g], N_OUT]),
                 op=ALU.add,
             )
-            nc.sync.dma_start(out=out_groups[g], in_=res[:].rearrange("p r n -> p (r n)"))
+            nc.sync.dma_start(
+                out=out[rows_of(g)].rearrange("(p r) n -> p (r n)", r=GROUPS[g]),
+                in_=res[:].rearrange("p r n -> p (r n)"),
+            )
 
-        def for_tile(stage, t):
-            if 0 <= t < TILES:
-                stage(t)
-
-        def for_group(stage, t):
-            if 0 <= t < TILES and t % SUB == SUB - 1:
-                stage(t // SUB)
-
-        with tc.manual_schedule():
-            for t in range(LOADS_AHEAD):
-                load(t)
-
-            ident = const.tile([P, P], F32)
-            make_identity(nc, ident[:])
-            one_col = const.tile([P, 1], F32)
-            nc.vector.memset(one_col[:], 1.0)
-
-            bias_bf = const.tile([P, N_OUT], BF16)
+        def load_bias():
             nc.sync.dma_start(out=bias_bf[:], in_=bc.partition_broadcast(P))
-            bias = const.tile([P, N_OUT], F32)
-            nc.vector.tensor_copy(out=bias[:], in_=bias_bf[:])
 
-            w_raw = const.tile([P, PASSES, 2 * HALVES, N_OUT], BF16)
+        def load_weights():
             nc.sync.dma_start(
                 out=w_raw[:].rearrange("q c t n -> q c (t n)"),
                 in_=Wc.rearrange("(c q t) n -> q c (t n)", q=P, t=2 * HALVES),
             )
-            w_grouped = const.tile([P, PASSES, N_OUT, 2 * HALVES], BF16, align_bytes=64)
+
+        def quantise_weights():
             nc.vector.tensor_copy(out=w_grouped[:], in_=w_raw[:].rearrange("q c t n -> q c n t"))
-            w_codes = const.tile([P, PASSES, N_OUT], U32, align_bytes=64)
-            w_scales = const.tile([P, PASSES, N_OUT], U8, align_bytes=64)
             nc.vector.quantize_mx(
                 out=w_codes[:].rearrange("q c n -> q (c n)").bitcast(FP8X4),
                 scales=w_scales[:].rearrange("q c n -> q (c n)"),
                 in_=w_grouped[:].rearrange("q c n t -> q (c n t)"),
             )
 
-            for step in range(TILES + LAG_FINISH):
-                for_tile(sums, step - LAG_SUMS)
-                for_group(factor, step - LAG_FACTOR)
-                for_group(denom, step - LAG_DENOM)
-                for_tile(scale, step - LAG_SCALE)
-                for_tile(transpose, step - LAG_TRANSPOSE)
-                for_tile(evacuate, step - LAG_EVACUATE)
-                for_group(quantise, step - LAG_QUANTISE)
-                for_group(multiply, step - LAG_MULTIPLY)
-                for_group(finish, step - LAG_FINISH)
-                for_group(recip, step - LAG_RECIP)
-                for_group(one_plus, step - LAG_ONE_PLUS)
-                for_tile(squares, step)
-                for_tile(load, step + LOADS_AHEAD)
+        def widen_bias():
+            nc.vector.tensor_copy(out=bias[:], in_=bias_bf[:])
+
+        calls = []
+
+        def at(due, stage, *what):
+            calls.append((due, len(calls), stage, what))
+
+        scale_due = []
+        for g, n in enumerate(GROUPS):
+            for r in range(n):
+                ready = FIRST[g] + n - 1 + 3.7 + r
+                scale_due.append(max(ready, scale_due[-1] + 1) if scale_due else ready)
+
+        for g, n in enumerate(GROUPS):
+            last = FIRST[g] + n - 1
+            at(-9 + 0.1 * g if g < LOADS_AHEAD + 1 else FIRST[g - LOADS_AHEAD] - 0.5, load, g)
+            for t in range(FIRST[g], last + 1):
+                at(t, squares, t)
+                at(t + 0.1, halve, t)
+                at(t + 1.3, sums, t)
+            at(last + 1.9, one_plus, g)
+            at(last + 2.2, denom, g)
+            at(last + 2.9, recip, g)
+            at(max(last + 3.2, scale_due[FIRST[g - 1] - 1] + 0.05 if g > 1 else 0), factor, g)
+            for t in range(FIRST[g], last + 1):
+                at(scale_due[t], scale, t)
+                at(scale_due[t] + 0.9, transpose, t)
+                at(scale_due[t] + 1.8, evacuate, t)
+            at(scale_due[last] + 2.6, quantise, g)
+            at(scale_due[last] + 2.7, multiply, g)
+            at(scale_due[last] + 3.6, finish, g)
+        at(-8.65, load_weights)
+        at(-8.4, load_bias)
+        at(3.3, quantise_weights)
+        at(3.4, widen_bias)
+
+        with tc.manual_schedule():
+            ident = const.tile([P, P], F32)
+            make_identity(nc, ident[:])
+            one_col = const.tile([P, 1], F32)
+            nc.vector.memset(one_col[:], 1.0)
+            warm = const.tile([P, 1], F32)
+            nc.scalar.activation(out=warm[:], in_=one_col[:], func=ACT.Abs_reciprocal_sqrt)
+            bias_bf = const.tile([P, N_OUT], BF16)
+            bias = const.tile([P, N_OUT], F32)
+            w_raw = const.tile([P, PASSES, 2 * HALVES, N_OUT], BF16)
+            w_grouped = const.tile([P, PASSES, N_OUT, 2 * HALVES], BF16, align_bytes=64)
+            w_codes = const.tile([P, PASSES, N_OUT], U32, align_bytes=64)
+            w_scales = const.tile([P, PASSES, N_OUT], U8, align_bytes=64)
+            for due, order, stage, what in sorted(calls, key=lambda call: call[:2]):
+                stage(*what)

@@ -23,13 +23,15 @@ TILES = ROWS // P
 PASSES = K // (4 * P)
 HALVES = 2
 
-MAX_GROUP = 4
-ENDS = [1, 1, 2]
-GROUPS = ENDS + [MAX_GROUP] * ((TILES - 2 * sum(ENDS)) // MAX_GROUP) + ENDS[::-1]
-FIRST = [sum(GROUPS[:g]) for g in range(len(GROUPS))]
-GROUP_OF = [g for g, n in enumerate(GROUPS) for r in range(n)]
+SUB = 2
+SPAN = 4
+GROUPS = TILES // SUB
 VECTOR_SQUARES = (1, 3)
-LOADS_AHEAD = 3
+GPSIMD_SQUARES = tuple(range(5, TILES, 2))
+GLEAD = 2.5
+L = 5.7
+GPSIMD_SCALES = ()
+LOADS_AHEAD = 4
 
 FLOPS = 2 * ROWS * K * N_OUT
 
@@ -38,9 +40,8 @@ def tile_capsulenetwork_pc_t_kernel(tc, s, Wc, bc, out):
     nc = tc.nc
     with ExitStack() as ctx:
         const = ctx.enter_context(tc.tile_pool(name="const", bufs=1))
-        x_pool = ctx.enter_context(tc.tile_pool(name="x", bufs=7))
-        sq_pool = ctx.enter_context(tc.tile_pool(name="sq", bufs=4))
-        hs_pool = ctx.enter_context(tc.tile_pool(name="hs", bufs=4))
+        x_pool = ctx.enter_context(tc.tile_pool(name="x", bufs=10))
+        sq_pool = ctx.enter_context(tc.tile_pool(name="sq", bufs=10))
         small = ctx.enter_context(tc.tile_pool(name="small", bufs=2))
         v_pool = ctx.enter_context(tc.tile_pool(name="v", bufs=4))
         mx_pool = ctx.enter_context(tc.tile_pool(name="mx", bufs=3))
@@ -52,7 +53,7 @@ def tile_capsulenetwork_pc_t_kernel(tc, s, Wc, bc, out):
 
         x_of = {}
         sq_of = {}
-        hs_of = {}
+        fsb_of = {}
         q_of = {}
         one_plus_of = {}
         denom_of = {}
@@ -65,93 +66,106 @@ def tile_capsulenetwork_pc_t_kernel(tc, s, Wc, bc, out):
         scales_of = {}
         acc_of = {}
 
-        def rows_of(g):
-            return slice(FIRST[g] * P, (FIRST[g] + GROUPS[g]) * P)
-
         def place(t):
-            return GROUP_OF[t], t - FIRST[GROUP_OF[t]]
+            return t // SUB, t % SUB
+
+        s_spans = s.rearrange("(h p r) j o -> h p r (j o)", p=P, r=SPAN)
+        out_spans = out.rearrange("(h p r) n -> h p (r n)", p=P, r=SPAN)
 
         def load(g):
-            x = x_pool.tile([P, GROUPS[g], CAPS, CAP_LEN], BF16)
+            x = x_pool.tile([P, SUB, CAPS, CAP_LEN], BF16)
             nc.sync.dma_start(
-                out=x[:].rearrange("p r j o -> p (r j o)"),
-                in_=s[rows_of(g)].rearrange("(p r) j o -> p (r j o)", r=GROUPS[g]),
+                out=x[:].rearrange("p r j o -> p r (j o)"),
+                in_=s_spans[SUB * g // SPAN][:, SUB * g % SPAN : SUB * g % SPAN + SUB],
             )
             x_of[g] = x
 
         def squares(t):
             g, r = place(t)
-            sq = sq_pool.tile([P, CAPS, CAP_LEN], F32)
-            if t in VECTOR_SQUARES:
-                nc.vector.tensor_tensor(out=sq[:], in0=x_of[g][:, r], in1=x_of[g][:, r], op=ALU.mult)
-            else:
-                nc.scalar.activation(out=sq[:], in_=x_of[g][:, r], func=ACT.Square)
+            sq = sq_pool.tile([P, CAP_LEN, CAPS], F32)
+            for first in range(0, CAP_LEN, HALF_CAP):
+                half = slice(first, first + HALF_CAP)
+                x_half = x_of[g][:, r, :, half]
+                sq_half = sq[:, half].rearrange("p d j -> p j d")
+                if t in VECTOR_SQUARES:
+                    nc.vector.tensor_tensor(out=sq_half, in0=x_half, in1=x_half, op=ALU.mult)
+                elif t in GPSIMD_SQUARES:
+                    nc.gpsimd.tensor_tensor(out=sq_half, in0=x_half, in1=x_half, op=ALU.mult)
+                else:
+                    nc.scalar.activation(out=sq_half, in_=x_half, func=ACT.Square)
             sq_of[t] = sq
-
-        def halve(t):
-            hs = hs_pool.tile([P, CAPS, HALF_CAP], F32)
-            nc.gpsimd.tensor_tensor(
-                out=hs[:],
-                in0=sq_of[t][:, :, 0:HALF_CAP],
-                in1=sq_of[t][:, :, HALF_CAP:CAP_LEN],
-                op=ALU.add,
-            )
-            hs_of[t] = hs
 
         def sums(t):
             g, r = place(t)
             if r == 0:
-                q_t = q_psum.tile([P, GROUPS[g], P], F32)
+                q_t = q_psum.tile([P, SPAN, P], F32)
                 q_of[g] = q_t
-            for d in range(HALF_CAP):
+            for d in range(CAP_LEN):
                 nc.tensor.matmul(
                     out=q_of[g][:, r, :],
-                    lhsT=hs_of[t][:, :, d],
+                    lhsT=sq_of[t][:, d, :],
                     rhs=ident[:],
                     is_transpose=True,
                     start=(d == 0),
-                    stop=(d == HALF_CAP - 1),
+                    stop=(d == CAP_LEN - 1),
                 )
 
         def one_plus(g):
-            one_plus_sq = small.tile([P, GROUPS[g], P], F32)
-            nc.scalar.activation(out=one_plus_sq[:], in_=q_of[g][:], func=ACT.Square, bias=one_col[:, 0:1])
+            one_plus_sq = small.tile([P, SUB, P], F32)
+            nc.scalar.activation(out=one_plus_sq[:], in_=q_of[g][:, :SUB], func=ACT.Square, bias=one_col[:, 0:1])
             one_plus_of[g] = one_plus_sq
 
         def denom(g):
-            denom_sq = small.tile([P, GROUPS[g], P], F32)
+            denom_sq = small.tile([P, SUB, P], F32)
             nc.vector.scalar_tensor_tensor(
-                out=denom_sq[:], in0=q_of[g][:], scalar=SQ_EPS, in1=one_plus_of[g][:], op0=ALU.add, op1=ALU.mult
+                out=denom_sq[:], in0=q_of[g][:, :SUB], scalar=SQ_EPS, in1=one_plus_of[g][:], op0=ALU.add, op1=ALU.mult
             )
             denom_of[g] = denom_sq
 
         def recip(g):
-            recip_t = small.tile([P, GROUPS[g], P], F32)
+            recip_t = small.tile([P, SUB, P], F32)
             nc.scalar.activation(out=recip_t[:], in_=denom_of[g][:], func=ACT.Abs_reciprocal_sqrt)
             recip_of[g] = recip_t
 
         def factor(g):
-            f_t = small.tile([P, GROUPS[g], P], F32)
-            nc.vector.tensor_tensor(out=f_t[:], in0=q_of[g][:], in1=recip_of[g][:], op=ALU.mult)
-            f_rows = f_psum.tile([P, GROUPS[g], CAPS], F32)
-            for r in range(GROUPS[g]):
+            f_t = small.tile([P, SUB, P], F32)
+            nc.vector.tensor_tensor(out=f_t[:], in0=q_of[g][:, :SUB], in1=recip_of[g][:], op=ALU.mult)
+            f_rows = f_psum.tile([P, SPAN, CAPS], F32)
+            for r in range(SUB):
                 nc.tensor.transpose(out=f_rows[:, r, :], in_=f_t[:, r, :], identity=ident[:])
             f_of[g] = f_rows
 
         def scale(t):
             g, r = place(t)
-            v = v_pool.tile([P, HALVES, CAPS, 2, 2], BF16)
+            v = v_pool.tile([P, HALVES, CAPS, HALF_CAP], BF16)
+            nc.vector.tensor_tensor(
+                out=v[:],
+                in0=x_of[g][:, r].rearrange("p j (u d) -> p u j d", u=HALVES),
+                in1=f_of[g][:, r, :].unsqueeze(1).unsqueeze(3).to_broadcast([P, HALVES, CAPS, HALF_CAP]),
+                op=ALU.mult,
+            )
+            v_of[t] = v
+
+        def copy_factor(t):
+            g, r = place(t)
+            f_sb = small.tile([P, CAPS], F32)
+            nc.scalar.copy(out=f_sb[:], in_=f_of[g][:, r, :])
+            fsb_of[t] = f_sb
+
+        def gpsimd_scale(t):
+            g, r = place(t)
+            v = v_pool.tile([P, HALVES, CAPS, HALF_CAP], BF16)
             for u in range(HALVES):
-                nc.vector.tensor_tensor(
+                nc.gpsimd.tensor_tensor(
                     out=v[:, u],
-                    in0=x_of[g][:, r].rearrange("p j (h u e) -> p u j h e", h=2, u=HALVES)[:, u],
-                    in1=f_of[g][:, r, :].unsqueeze(2).unsqueeze(3).to_broadcast([P, CAPS, 2, 2]),
+                    in0=x_of[g][:, r, :, u * HALF_CAP : (u + 1) * HALF_CAP],
+                    in1=fsb_of[t][:].unsqueeze(2).to_broadcast([P, CAPS, HALF_CAP]),
                     op=ALU.mult,
                 )
             v_of[t] = v
 
         def transpose(t):
-            v_words = v_of[t][:].rearrange("p u j h e -> p (u j h e)").bitcast(F32)
+            v_words = v_of[t][:].rearrange("p u j d -> p (u j d)").bitcast(F32)
             v_t = t_psum.tile([P, PASSES, HALVES, P], F32)
             for c in range(PASSES):
                 for u in range(HALVES):
@@ -162,59 +176,59 @@ def tile_capsulenetwork_pc_t_kernel(tc, s, Wc, bc, out):
             vt_of[t] = v_t
 
         def evacuate(t):
-            g, r = place(t)
-            if r == 0:
-                grouped = mx_pool.tile([P, GROUPS[g], PASSES, P, HALVES], F32, align_bytes=64)
-                grouped_of[g] = grouped
-            nc.scalar.copy(out=grouped_of[g][:, r], in_=vt_of[t][:].rearrange("q c u p -> q c p u"))
+            if t % SPAN == 0:
+                grouped = mx_pool.tile([P, SPAN, PASSES, P, HALVES], F32, align_bytes=64)
+                grouped_of[t // SPAN] = grouped
+            nc.scalar.copy(
+                out=grouped_of[t // SPAN][:, t % SPAN], in_=vt_of[t][:].rearrange("q c u p -> q c p u")
+            )
 
-        def quantise(g):
-            codes = mx_pool.tile([P, GROUPS[g], PASSES, P], U32, align_bytes=64)
-            scales = mx_pool.tile([P, GROUPS[g], PASSES, P], U8, align_bytes=64)
+        def quantise(h):
+            codes = mx_pool.tile([P, SPAN, PASSES, P], U32, align_bytes=64)
+            scales = mx_pool.tile([P, SPAN, PASSES, P], U8, align_bytes=64)
             nc.vector.quantize_mx(
                 out=codes[:].rearrange("q r c p -> q (r c p)").bitcast(FP8X4),
                 scales=scales[:].rearrange("q r c p -> q (r c p)"),
-                in_=grouped_of[g][:].rearrange("q r c p u -> q (r c p u)").bitcast(BF16),
+                in_=grouped_of[h][:].rearrange("q r c p u -> q (r c p u)").bitcast(BF16),
             )
-            codes_of[g] = codes
-            scales_of[g] = scales
+            codes_of[h] = codes
+            scales_of[h] = scales
 
-        def multiply(g):
-            acc = o_psum.tile([P, GROUPS[g], N_OUT], F32)
-            for r in range(GROUPS[g]):
+        def multiply(h):
+            acc = o_psum.tile([P, SPAN, N_OUT], F32)
+            for r in range(SPAN):
                 for c in range(PASSES):
                     nc.tensor.matmul_mx(
                         out=acc[:, r, :],
-                        lhsT=codes_of[g][:, r, c, :].bitcast(FP8X4),
-                        lhsT_scale=scales_of[g][:, r, c, :],
+                        lhsT=codes_of[h][:, r, c, :].bitcast(FP8X4),
+                        lhsT_scale=scales_of[h][:, r, c, :],
                         rhs=w_codes[:, c, :].bitcast(FP8X4),
                         rhs_scale=w_scales[:, c, :],
                         start=(c == 0),
                         stop=(c == PASSES - 1),
                     )
-            acc_of[g] = acc
+            acc_of[h] = acc
 
-        def finish(g):
-            res = res_pool.tile([P, GROUPS[g], N_OUT], F32)
+        def finish(h):
+            res = res_pool.tile([P, SPAN, N_OUT], F32)
             nc.vector.tensor_tensor(
                 out=res[:],
-                in0=acc_of[g][:],
-                in1=bias[:].unsqueeze(1).to_broadcast([P, GROUPS[g], N_OUT]),
+                in0=acc_of[h][:],
+                in1=bias[:].unsqueeze(1).to_broadcast([P, SPAN, N_OUT]),
                 op=ALU.add,
             )
-            nc.sync.dma_start(
-                out=out[rows_of(g)].rearrange("(p r) n -> p (r n)", r=GROUPS[g]),
-                in_=res[:].rearrange("p r n -> p (r n)"),
-            )
+            nc.sync.dma_start(out=out_spans[h], in_=res[:].rearrange("p r n -> p (r n)"))
 
         def load_bias():
             nc.sync.dma_start(out=bias_bf[:], in_=bc.partition_broadcast(P))
 
         def load_weights():
-            nc.sync.dma_start(
-                out=w_raw[:].rearrange("q c t n -> q c (t n)"),
-                in_=Wc.rearrange("(c q t) n -> q c (t n)", q=P, t=2 * HALVES),
-            )
+            rows = Wc.rearrange("(c j u i e) n -> c i j u (e n)", c=PASSES, u=HALVES, i=2, e=2)
+            for c in range(PASSES):
+                for i in range(2):
+                    nc.sync.dma_start(
+                        out=w_raw[i:P:2, c].rearrange("q (u e) n -> q u (e n)", u=HALVES), in_=rows[c, i]
+                    )
 
         def quantise_weights():
             nc.vector.tensor_copy(out=w_grouped[:], in_=w_raw[:].rearrange("q c t n -> q c n t"))
@@ -232,30 +246,29 @@ def tile_capsulenetwork_pc_t_kernel(tc, s, Wc, bc, out):
         def at(due, stage, *what):
             calls.append((due, len(calls), stage, what))
 
-        scale_due = []
-        for g, n in enumerate(GROUPS):
-            for r in range(n):
-                ready = FIRST[g] + n - 1 + 3.7 + r
-                scale_due.append(max(ready, scale_due[-1] + 1) if scale_due else ready)
-
-        for g, n in enumerate(GROUPS):
-            last = FIRST[g] + n - 1
-            at(-9 + 0.1 * g if g < LOADS_AHEAD + 1 else FIRST[g - LOADS_AHEAD] - 0.5, load, g)
-            for t in range(FIRST[g], last + 1):
-                at(t, squares, t)
-                at(t + 0.1, halve, t)
-                at(t + 1.3, sums, t)
-            at(last + 1.9, one_plus, g)
-            at(last + 2.2, denom, g)
-            at(last + 2.9, recip, g)
-            at(max(last + 3.2, scale_due[FIRST[g - 1] - 1] + 0.05 if g > 1 else 0), factor, g)
-            for t in range(FIRST[g], last + 1):
-                at(scale_due[t], scale, t)
-                at(scale_due[t] + 0.9, transpose, t)
-                at(scale_due[t] + 1.8, evacuate, t)
-            at(scale_due[last] + 2.6, quantise, g)
-            at(scale_due[last] + 2.7, multiply, g)
-            at(scale_due[last] + 3.6, finish, g)
+        for g in range(GROUPS):
+            a = SUB * g
+            at(-9 + 0.1 * g if g < LOADS_AHEAD + 1 else a - SUB * LOADS_AHEAD - 0.5, load, g)
+            for t in (a, a + 1):
+                at(t - GLEAD if t in GPSIMD_SQUARES else t, squares, t)
+            for t in (a, a + 1):
+                at((a if t in GPSIMD_SQUARES else t) + 0.85, sums, t)
+            at(a + L - 3.0, one_plus, g)
+            at(a + L - 2.8, denom, g)
+            at(a + L - 2.4, recip, g)
+            at(a + L - 1.6, factor, g)
+            for t, due in ((a, a + L), (a + 1, a + L + 0.8)):
+                if t in GPSIMD_SCALES:
+                    at(due - 0.5, copy_factor, t)
+                    at(due - 0.4, gpsimd_scale, t)
+                else:
+                    at(due, scale, t)
+                at(due + 0.35, transpose, t)
+                at(due + 1.2, evacuate, t)
+            if a % SPAN == SPAN - SUB:
+                at(a + L + 3.3, quantise, a // SPAN)
+                at(a + L + 3.4, multiply, a // SPAN)
+                at(a + L + 5.3, finish, a // SPAN)
         at(-8.65, load_weights)
         at(-8.4, load_bias)
         at(3.3, quantise_weights)

@@ -23,15 +23,16 @@ TILES = ROWS // P
 PASSES = K // (4 * P)
 HALVES = 2
 
-SUB = 2
-SPAN = 4
-GROUPS = TILES // SUB
-VECTOR_SQUARES = (1, 3)
-GPSIMD_SQUARES = tuple(range(5, TILES, 2))
-GLEAD = 2.5
-L = 5.7
-GPSIMD_SCALES = ()
-LOADS_AHEAD = 4
+HEAD = [2, 2]
+TAIL = [2, 2]
+MAX_GROUP = 4
+GROUPS = HEAD + [MAX_GROUP] * ((TILES - sum(HEAD) - sum(TAIL)) // MAX_GROUP) + TAIL
+FIRST = [sum(GROUPS[:g]) for g in range(len(GROUPS))]
+VECTOR_SQUARES = (1, 7)
+GPSIMD_HEAD_SQUARES = (3,)
+E_PERIOD = 2
+E_TAIL = 3
+LOADS_AHEAD = 3
 
 FLOPS = 2 * ROWS * K * N_OUT
 
@@ -40,19 +41,19 @@ def tile_capsulenetwork_pc_t_kernel(tc, s, Wc, bc, out):
     nc = tc.nc
     with ExitStack() as ctx:
         const = ctx.enter_context(tc.tile_pool(name="const", bufs=1))
-        x_pool = ctx.enter_context(tc.tile_pool(name="x", bufs=10))
+        x_pool = ctx.enter_context(tc.tile_pool(name="x", bufs=7))
         sq_pool = ctx.enter_context(tc.tile_pool(name="sq", bufs=10))
         small = ctx.enter_context(tc.tile_pool(name="small", bufs=2))
         v_pool = ctx.enter_context(tc.tile_pool(name="v", bufs=4))
         mx_pool = ctx.enter_context(tc.tile_pool(name="mx", bufs=3))
         res_pool = ctx.enter_context(tc.tile_pool(name="res", bufs=2))
         q_psum = ctx.enter_context(tc.psum_pool(name="q_psum", bufs=2))
-        f_psum = ctx.enter_context(tc.psum_pool(name="f_psum", bufs=2))
-        t_psum = ctx.enter_context(tc.psum_pool(name="t_psum", bufs=3))
+        f_psum = ctx.enter_context(tc.psum_pool(name="f_psum", bufs=1))
+        t_psum = ctx.enter_context(tc.psum_pool(name="t_psum", bufs=4))
         o_psum = ctx.enter_context(tc.psum_pool(name="o_psum", bufs=1))
 
         x_of = {}
-        sq_of = {}
+        planes_of = {}
         fsb_of = {}
         q_of = {}
         one_plus_of = {}
@@ -65,78 +66,87 @@ def tile_capsulenetwork_pc_t_kernel(tc, s, Wc, bc, out):
         codes_of = {}
         scales_of = {}
         acc_of = {}
+        acc_sb_of = {}
 
-        def place(t):
-            return t // SUB, t % SUB
-
-        s_spans = s.rearrange("(h p r) j o -> h p r (j o)", p=P, r=SPAN)
-        out_spans = out.rearrange("(h p r) n -> h p (r n)", p=P, r=SPAN)
+        def rows_of(g):
+            return slice(FIRST[g] * P, (FIRST[g] + GROUPS[g]) * P)
 
         def load(g):
-            x = x_pool.tile([P, SUB, CAPS, CAP_LEN], BF16)
+            x = x_pool.tile([P, GROUPS[g], CAPS, CAP_LEN], BF16)
             nc.sync.dma_start(
-                out=x[:].rearrange("p r j o -> p r (j o)"),
-                in_=s_spans[SUB * g // SPAN][:, SUB * g % SPAN : SUB * g % SPAN + SUB],
+                out=x[:].rearrange("p r j o -> p (r j o)"),
+                in_=s[rows_of(g)].rearrange("(p r) j o -> p (r j o)", r=GROUPS[g]),
             )
             x_of[g] = x
 
-        def squares(t):
-            g, r = place(t)
-            sq = sq_pool.tile([P, CAP_LEN, CAPS], F32)
-            for first in range(0, CAP_LEN, HALF_CAP):
-                half = slice(first, first + HALF_CAP)
-                x_half = x_of[g][:, r, :, half]
-                sq_half = sq[:, half].rearrange("p d j -> p j d")
-                if t in VECTOR_SQUARES:
-                    nc.vector.tensor_tensor(out=sq_half, in0=x_half, in1=x_half, op=ALU.mult)
-                elif t in GPSIMD_SQUARES:
-                    nc.gpsimd.tensor_tensor(out=sq_half, in0=x_half, in1=x_half, op=ALU.mult)
-                else:
-                    nc.scalar.activation(out=sq_half, in_=x_half, func=ACT.Square)
-            sq_of[t] = sq
+        def on_gpsimd(g, r):
+            t = FIRST[g] + r
+            return t in GPSIMD_HEAD_SQUARES or GROUPS[g] == MAX_GROUP and r % 2 == 1 and t not in VECTOR_SQUARES
 
-        def sums(t):
-            g, r = place(t)
-            if r == 0:
-                q_t = q_psum.tile([P, SPAN, P], F32)
+        def scaled_on_gpsimd(g, r):
+            if g < 3 or GROUPS[g] < MAX_GROUP:
+                return False
+            return r == 3 and g % E_PERIOD == 0 or r >= 2 and g >= len(GROUPS) - len(TAIL) - E_TAIL
+
+        def squares(g, r):
+            x = x_of[g][:, r]
+            if on_gpsimd(g, r):
+                sq = sq_pool.tile([P, CAPS, CAP_LEN], F32)
+                for first in range(0, CAPS, CAPS // 2):
+                    part = slice(first, first + CAPS // 2)
+                    nc.gpsimd.tensor_tensor(out=sq[:, part], in0=x[:, part], in1=x[:, part], op=ALU.mult)
+                planes_of[g, r] = [sq[:, :, o] for o in range(CAP_LEN)]
+            else:
+                sq_planes = sq_pool.tile([P, CAP_LEN, CAPS], F32)
+                for first in range(0, CAP_LEN, HALF_CAP):
+                    part = slice(first, first + HALF_CAP)
+                    out_part = sq_planes[:, part].rearrange("p o j -> p j o")
+                    if FIRST[g] + r in VECTOR_SQUARES:
+                        nc.vector.tensor_tensor(out=out_part, in0=x[:, :, part], in1=x[:, :, part], op=ALU.mult)
+                    else:
+                        nc.scalar.activation(out=out_part, in_=x[:, :, part], func=ACT.Square)
+                planes_of[g, r] = [sq_planes[:, o, :] for o in range(CAP_LEN)]
+
+        def sums(g, r, planes=range(CAP_LEN)):
+            if g not in q_of:
+                q_t = q_psum.tile([P, MAX_GROUP, P], F32)
                 q_of[g] = q_t
-            for d in range(CAP_LEN):
+            for o in planes:
                 nc.tensor.matmul(
                     out=q_of[g][:, r, :],
-                    lhsT=sq_of[t][:, d, :],
+                    lhsT=planes_of[g, r][o],
                     rhs=ident[:],
                     is_transpose=True,
-                    start=(d == 0),
-                    stop=(d == CAP_LEN - 1),
+                    start=(o == 0),
+                    stop=(o == CAP_LEN - 1),
                 )
 
         def one_plus(g):
-            one_plus_sq = small.tile([P, SUB, P], F32)
-            nc.scalar.activation(out=one_plus_sq[:], in_=q_of[g][:, :SUB], func=ACT.Square, bias=one_col[:, 0:1])
+            one_plus_sq = small.tile([P, GROUPS[g], P], F32)
+            nc.scalar.activation(out=one_plus_sq[:], in_=q_of[g][:, : GROUPS[g]], func=ACT.Square, bias=one_col[:, 0:1])
             one_plus_of[g] = one_plus_sq
 
         def denom(g):
-            denom_sq = small.tile([P, SUB, P], F32)
+            denom_sq = small.tile([P, GROUPS[g], P], F32)
             nc.vector.scalar_tensor_tensor(
-                out=denom_sq[:], in0=q_of[g][:, :SUB], scalar=SQ_EPS, in1=one_plus_of[g][:], op0=ALU.add, op1=ALU.mult
+                out=denom_sq[:], in0=q_of[g][:, : GROUPS[g]], scalar=SQ_EPS, in1=one_plus_of[g][:], op0=ALU.add, op1=ALU.mult
             )
             denom_of[g] = denom_sq
 
         def recip(g):
-            recip_t = small.tile([P, SUB, P], F32)
+            recip_t = small.tile([P, GROUPS[g], P], F32)
             nc.scalar.activation(out=recip_t[:], in_=denom_of[g][:], func=ACT.Abs_reciprocal_sqrt)
             recip_of[g] = recip_t
 
         def factor(g):
-            f_t = small.tile([P, SUB, P], F32)
-            nc.vector.tensor_tensor(out=f_t[:], in0=q_of[g][:, :SUB], in1=recip_of[g][:], op=ALU.mult)
-            f_rows = f_psum.tile([P, SPAN, CAPS], F32)
-            for r in range(SUB):
+            f_t = small.tile([P, GROUPS[g], P], F32)
+            nc.vector.tensor_tensor(out=f_t[:], in0=q_of[g][:, : GROUPS[g]], in1=recip_of[g][:], op=ALU.mult)
+            f_rows = f_psum.tile([P, MAX_GROUP, CAPS], F32)
+            for r in range(GROUPS[g]):
                 nc.tensor.transpose(out=f_rows[:, r, :], in_=f_t[:, r, :], identity=ident[:])
             f_of[g] = f_rows
 
-        def scale(t):
-            g, r = place(t)
+        def scale(g, r):
             v = v_pool.tile([P, HALVES, CAPS, HALF_CAP], BF16)
             nc.vector.tensor_tensor(
                 out=v[:],
@@ -144,28 +154,26 @@ def tile_capsulenetwork_pc_t_kernel(tc, s, Wc, bc, out):
                 in1=f_of[g][:, r, :].unsqueeze(1).unsqueeze(3).to_broadcast([P, HALVES, CAPS, HALF_CAP]),
                 op=ALU.mult,
             )
-            v_of[t] = v
+            v_of[g, r] = v
 
-        def copy_factor(t):
-            g, r = place(t)
+        def copy_factor(g, r):
             f_sb = small.tile([P, CAPS], F32)
             nc.scalar.copy(out=f_sb[:], in_=f_of[g][:, r, :])
-            fsb_of[t] = f_sb
+            fsb_of[g, r] = f_sb
 
-        def gpsimd_scale(t):
-            g, r = place(t)
+        def gpsimd_scale(g, r):
             v = v_pool.tile([P, HALVES, CAPS, HALF_CAP], BF16)
             for u in range(HALVES):
                 nc.gpsimd.tensor_tensor(
                     out=v[:, u],
                     in0=x_of[g][:, r, :, u * HALF_CAP : (u + 1) * HALF_CAP],
-                    in1=fsb_of[t][:].unsqueeze(2).to_broadcast([P, CAPS, HALF_CAP]),
+                    in1=fsb_of[g, r][:].unsqueeze(2).to_broadcast([P, CAPS, HALF_CAP]),
                     op=ALU.mult,
                 )
-            v_of[t] = v
+            v_of[g, r] = v
 
-        def transpose(t):
-            v_words = v_of[t][:].rearrange("p u j d -> p (u j d)").bitcast(F32)
+        def transpose(g, r):
+            v_words = v_of[g, r][:].rearrange("p u j d -> p (u j d)").bitcast(F32)
             v_t = t_psum.tile([P, PASSES, HALVES, P], F32)
             for c in range(PASSES):
                 for u in range(HALVES):
@@ -173,51 +181,52 @@ def tile_capsulenetwork_pc_t_kernel(tc, s, Wc, bc, out):
                     nc.tensor.transpose(
                         out=v_t[:, c, u, :], in_=v_words[:, first : first + P], identity=ident[:]
                     )
-            vt_of[t] = v_t
+            vt_of[g, r] = v_t
 
-        def evacuate(t):
-            if t % SPAN == 0:
-                grouped = mx_pool.tile([P, SPAN, PASSES, P, HALVES], F32, align_bytes=64)
-                grouped_of[t // SPAN] = grouped
-            nc.scalar.copy(
-                out=grouped_of[t // SPAN][:, t % SPAN], in_=vt_of[t][:].rearrange("q c u p -> q c p u")
-            )
+        def evacuate(g, r):
+            if r == 0:
+                grouped = mx_pool.tile([P, GROUPS[g], PASSES, P, HALVES], F32, align_bytes=64)
+                grouped_of[g] = grouped
+            nc.scalar.copy(out=grouped_of[g][:, r], in_=vt_of[g, r][:].rearrange("q c u p -> q c p u"))
 
-        def quantise(h):
-            codes = mx_pool.tile([P, SPAN, PASSES, P], U32, align_bytes=64)
-            scales = mx_pool.tile([P, SPAN, PASSES, P], U8, align_bytes=64)
+        def quantise(g):
+            codes = mx_pool.tile([P, GROUPS[g], PASSES, P], U32, align_bytes=64)
+            scales = mx_pool.tile([P, GROUPS[g], PASSES, P], U8, align_bytes=64)
             nc.vector.quantize_mx(
                 out=codes[:].rearrange("q r c p -> q (r c p)").bitcast(FP8X4),
                 scales=scales[:].rearrange("q r c p -> q (r c p)"),
-                in_=grouped_of[h][:].rearrange("q r c p u -> q (r c p u)").bitcast(BF16),
+                in_=grouped_of[g][:].rearrange("q r c p u -> q (r c p u)").bitcast(BF16),
             )
-            codes_of[h] = codes
-            scales_of[h] = scales
+            codes_of[g] = codes
+            scales_of[g] = scales
 
-        def multiply(h):
-            acc = o_psum.tile([P, SPAN, N_OUT], F32)
-            for r in range(SPAN):
+        def multiply(g):
+            acc = o_psum.tile([P, MAX_GROUP, N_OUT], F32)
+            for r in range(GROUPS[g]):
                 for c in range(PASSES):
                     nc.tensor.matmul_mx(
                         out=acc[:, r, :],
-                        lhsT=codes_of[h][:, r, c, :].bitcast(FP8X4),
-                        lhsT_scale=scales_of[h][:, r, c, :],
+                        lhsT=codes_of[g][:, r, c, :].bitcast(FP8X4),
+                        lhsT_scale=scales_of[g][:, r, c, :],
                         rhs=w_codes[:, c, :].bitcast(FP8X4),
                         rhs_scale=w_scales[:, c, :],
                         start=(c == 0),
                         stop=(c == PASSES - 1),
                     )
-            acc_of[h] = acc
+            acc_of[g] = acc
 
-        def finish(h):
-            res = res_pool.tile([P, SPAN, N_OUT], F32)
+        def finish(g):
+            res = res_pool.tile([P, GROUPS[g], N_OUT], F32)
             nc.vector.tensor_tensor(
                 out=res[:],
-                in0=acc_of[h][:],
-                in1=bias[:].unsqueeze(1).to_broadcast([P, SPAN, N_OUT]),
+                in0=acc_of[g][:, : GROUPS[g]],
+                in1=bias[:].unsqueeze(1).to_broadcast([P, GROUPS[g], N_OUT]),
                 op=ALU.add,
             )
-            nc.sync.dma_start(out=out_spans[h], in_=res[:].rearrange("p r n -> p (r n)"))
+            nc.sync.dma_start(
+                out=out[rows_of(g)].rearrange("(p r) n -> p (r n)", r=GROUPS[g]),
+                in_=res[:].rearrange("p r n -> p (r n)"),
+            )
 
         def load_bias():
             nc.sync.dma_start(out=bias_bf[:], in_=bc.partition_broadcast(P))
@@ -241,38 +250,42 @@ def tile_capsulenetwork_pc_t_kernel(tc, s, Wc, bc, out):
         def widen_bias():
             nc.vector.tensor_copy(out=bias[:], in_=bias_bf[:])
 
-        calls = []
+        def group_stage(stage, g):
+            if 0 <= g < len(GROUPS):
+                stage(g)
 
-        def at(due, stage, *what):
-            calls.append((due, len(calls), stage, what))
+        def tile_stage(stage, g, r, *more):
+            if 0 <= g < len(GROUPS) and r < GROUPS[g]:
+                stage(g, r, *more)
 
-        for g in range(GROUPS):
-            a = SUB * g
-            at(-9 + 0.1 * g if g < LOADS_AHEAD + 1 else a - SUB * LOADS_AHEAD - 0.5, load, g)
-            for t in (a, a + 1):
-                at(t - GLEAD if t in GPSIMD_SQUARES else t, squares, t)
-            for t in (a, a + 1):
-                at((a if t in GPSIMD_SQUARES else t) + 0.85, sums, t)
-            at(a + L - 3.0, one_plus, g)
-            at(a + L - 2.8, denom, g)
-            at(a + L - 2.4, recip, g)
-            at(a + L - 1.6, factor, g)
-            for t, due in ((a, a + L), (a + 1, a + L + 0.8)):
-                if t in GPSIMD_SCALES:
-                    at(due - 0.5, copy_factor, t)
-                    at(due - 0.4, gpsimd_scale, t)
-                else:
-                    at(due, scale, t)
-                at(due + 0.35, transpose, t)
-                at(due + 1.2, evacuate, t)
-            if a % SPAN == SPAN - SUB:
-                at(a + L + 3.3, quantise, a // SPAN)
-                at(a + L + 3.4, multiply, a // SPAN)
-                at(a + L + 5.3, finish, a // SPAN)
-        at(-8.65, load_weights)
-        at(-8.4, load_bias)
-        at(3.3, quantise_weights)
-        at(3.4, widen_bias)
+        def period(p):
+            group_stage(load, p + 3 + LOADS_AHEAD)
+            for r in range(MAX_GROUP):
+                if p < len(GROUPS) and r < GROUPS[p] and scaled_on_gpsimd(p, r):
+                    copy_factor(p, r)
+                    gpsimd_scale(p, r)
+            group_stage(one_plus, p + 1)
+            tile_stage(sums, p + 2, 0)
+            for r in range(MAX_GROUP):
+                if p < len(GROUPS) and r < GROUPS[p] and not scaled_on_gpsimd(p, r):
+                    scale(p, r)
+                tile_stage(squares, p + 3, r)
+                tile_stage(transpose, p, r)
+                if r == 0:
+                    tile_stage(sums, p + 2, 2)
+                if r == 1:
+                    tile_stage(sums, p + 2, 1)
+                if r == 2:
+                    tile_stage(sums, p + 2, 3, range(HALF_CAP))
+                if r == 1:
+                    group_stage(denom, p + 1)
+                    group_stage(recip, p + 1)
+                tile_stage(evacuate, p, r)
+            group_stage(factor, p + 1)
+            tile_stage(sums, p + 2, 3, range(HALF_CAP, CAP_LEN))
+            group_stage(quantise, p - 1)
+            group_stage(multiply, p - 1)
+            group_stage(finish, p - 2)
 
         with tc.manual_schedule():
             ident = const.tile([P, P], F32)
@@ -287,5 +300,28 @@ def tile_capsulenetwork_pc_t_kernel(tc, s, Wc, bc, out):
             w_grouped = const.tile([P, PASSES, N_OUT, 2 * HALVES], BF16, align_bytes=64)
             w_codes = const.tile([P, PASSES, N_OUT], U32, align_bytes=64)
             w_scales = const.tile([P, PASSES, N_OUT], U8, align_bytes=64)
-            for due, order, stage, what in sorted(calls, key=lambda call: call[:2]):
-                stage(*what)
+            load(0)
+            load(1)
+            load(2)
+            load_weights()
+            load_bias()
+            for g in range(3, 3 + LOADS_AHEAD):
+                load(g)
+            squares(0, 0)
+            squares(0, 1)
+            squares(1, 0)
+            squares(1, 1)
+            sums(0, 0)
+            sums(0, 1)
+            one_plus(0)
+            denom(0)
+            recip(0)
+            sums(1, 0)
+            sums(1, 1)
+            factor(0)
+            for r in range(GROUPS[2]):
+                squares(2, r)
+            quantise_weights()
+            widen_bias()
+            for p in range(len(GROUPS) + 2):
+                period(p)

@@ -28,10 +28,13 @@ TAIL = [2, 2]
 MAX_GROUP = 4
 GROUPS = HEAD + [MAX_GROUP] * ((TILES - sum(HEAD) - sum(TAIL)) // MAX_GROUP) + TAIL
 FIRST = [sum(GROUPS[:g]) for g in range(len(GROUPS))]
-VECTOR_SQUARES = (1, 7)
-GPSIMD_HEAD_SQUARES = (3,)
-E_PERIOD = 2
-E_TAIL = 3
+VECTOR_SQUARES = (1, 3, 5, 7, 9)
+GPSIMD_HEAD_SQUARES = ()
+E_PERIOD = 1000
+E_TAIL = 2
+HOLD_FROM = 1
+WPREP = 1
+SCALAR_SQUARES = ()
 LOADS_AHEAD = 3
 
 FLOPS = 2 * ROWS * K * N_OUT
@@ -43,7 +46,7 @@ def tile_capsulenetwork_pc_t_kernel(tc, s, Wc, bc, out):
         const = ctx.enter_context(tc.tile_pool(name="const", bufs=1))
         x_pool = ctx.enter_context(tc.tile_pool(name="x", bufs=7))
         sq_pool = ctx.enter_context(tc.tile_pool(name="sq", bufs=10))
-        small = ctx.enter_context(tc.tile_pool(name="small", bufs=2))
+        small = ctx.enter_context(tc.tile_pool(name="small", bufs=3))
         v_pool = ctx.enter_context(tc.tile_pool(name="v", bufs=4))
         mx_pool = ctx.enter_context(tc.tile_pool(name="mx", bufs=3))
         res_pool = ctx.enter_context(tc.tile_pool(name="res", bufs=2))
@@ -73,20 +76,22 @@ def tile_capsulenetwork_pc_t_kernel(tc, s, Wc, bc, out):
 
         def load(g):
             x = x_pool.tile([P, GROUPS[g], CAPS, CAP_LEN], BF16)
-            nc.sync.dma_start(
-                out=x[:].rearrange("p r j o -> p (r j o)"),
-                in_=s[rows_of(g)].rearrange("(p r) j o -> p (r j o)", r=GROUPS[g]),
-            )
+            rows = s[rows_of(g)].rearrange("(p r) j o -> p r (j o)", r=GROUPS[g])
+            step = 1 if g < 2 else 2 if g == 2 else GROUPS[g]
+            for r in range(0, GROUPS[g], step):
+                nc.sync.dma_start(
+                    out=x[:, r : r + step].rearrange("p r j o -> p r (j o)"), in_=rows[:, r : r + step]
+                )
             x_of[g] = x
 
         def on_gpsimd(g, r):
             t = FIRST[g] + r
-            return t in GPSIMD_HEAD_SQUARES or GROUPS[g] == MAX_GROUP and r % 2 == 1 and t not in VECTOR_SQUARES
+            return t in GPSIMD_HEAD_SQUARES or GROUPS[g] == MAX_GROUP and r % 2 == 1 and t not in VECTOR_SQUARES + SCALAR_SQUARES
 
         def scaled_on_gpsimd(g, r):
             if g < 3 or GROUPS[g] < MAX_GROUP:
                 return False
-            return r == 3 and g % E_PERIOD == 0 or r >= 2 and g >= len(GROUPS) - len(TAIL) - E_TAIL
+            return r == 3 and g >= len(GROUPS) - len(TAIL) - E_TAIL
 
         def squares(g, r):
             x = x_of[g][:, r]
@@ -107,11 +112,11 @@ def tile_capsulenetwork_pc_t_kernel(tc, s, Wc, bc, out):
                         nc.scalar.activation(out=out_part, in_=x[:, :, part], func=ACT.Square)
                 planes_of[g, r] = [sq_planes[:, o, :] for o in range(CAP_LEN)]
 
-        def sums(g, r, planes=range(CAP_LEN)):
+        def sums(g, r, half=None):
             if g not in q_of:
                 q_t = q_psum.tile([P, MAX_GROUP, P], F32)
                 q_of[g] = q_t
-            for o in planes:
+            for o in range(CAP_LEN) if half is None else range(half * HALF_CAP, (half + 1) * HALF_CAP):
                 nc.tensor.matmul(
                     out=q_of[g][:, r, :],
                     lhsT=planes_of[g, r][o],
@@ -133,6 +138,10 @@ def tile_capsulenetwork_pc_t_kernel(tc, s, Wc, bc, out):
             )
             denom_of[g] = denom_sq
 
+        def hold_gpsimd(g):
+            token = small.tile([P, 1], F32)
+            nc.gpsimd.tensor_copy(out=token[:], in_=denom_of[g][:, 0, 0:1])
+
         def recip(g):
             recip_t = small.tile([P, GROUPS[g], P], F32)
             nc.scalar.activation(out=recip_t[:], in_=denom_of[g][:], func=ACT.Abs_reciprocal_sqrt)
@@ -140,7 +149,7 @@ def tile_capsulenetwork_pc_t_kernel(tc, s, Wc, bc, out):
 
         def factor(g):
             f_t = small.tile([P, GROUPS[g], P], F32)
-            nc.vector.tensor_tensor(out=f_t[:], in0=q_of[g][:, : GROUPS[g]], in1=recip_of[g][:], op=ALU.mult)
+            nc.vector.tensor_tensor(out=f_t[:], in0=recip_of[g][:], in1=q_of[g][:, : GROUPS[g]], op=ALU.mult)
             f_rows = f_psum.tile([P, MAX_GROUP, CAPS], F32)
             for r in range(GROUPS[g]):
                 nc.tensor.transpose(out=f_rows[:, r, :], in_=f_t[:, r, :], identity=ident[:])
@@ -219,8 +228,8 @@ def tile_capsulenetwork_pc_t_kernel(tc, s, Wc, bc, out):
             res = res_pool.tile([P, GROUPS[g], N_OUT], F32)
             nc.vector.tensor_tensor(
                 out=res[:],
-                in0=acc_of[g][:, : GROUPS[g]],
-                in1=bias[:].unsqueeze(1).to_broadcast([P, GROUPS[g], N_OUT]),
+                in0=bias[:].unsqueeze(1).to_broadcast([P, GROUPS[g], N_OUT]),
+                in1=acc_of[g][:, : GROUPS[g]],
                 op=ALU.add,
             )
             nc.sync.dma_start(
@@ -250,42 +259,54 @@ def tile_capsulenetwork_pc_t_kernel(tc, s, Wc, bc, out):
         def widen_bias():
             nc.vector.tensor_copy(out=bias[:], in_=bias_bf[:])
 
+        done = set()
+
         def group_stage(stage, g):
-            if 0 <= g < len(GROUPS):
+            if 0 <= g < len(GROUPS) and (stage, g) not in done:
+                done.add((stage, g))
                 stage(g)
 
         def tile_stage(stage, g, r, *more):
-            if 0 <= g < len(GROUPS) and r < GROUPS[g]:
+            if 0 <= g < len(GROUPS) and r < GROUPS[g] and (stage, g, r) not in done and (stage, g, r, *more) not in done:
+                done.add((stage, g, r, *more))
                 stage(g, r, *more)
+
+        def all_tiles(stage, g):
+            for r in range(GROUPS[g]):
+                tile_stage(stage, g, r)
 
         def period(p):
             group_stage(load, p + 3 + LOADS_AHEAD)
+            if 0 <= p < len(GROUPS):
+                for r in range(GROUPS[p]):
+                    if scaled_on_gpsimd(p, r):
+                        copy_factor(p, r)
+                        gpsimd_scale(p, r)
+            group_stage(recip, p + 1)
+            tile_stage(sums, p + 2, 3)
             for r in range(MAX_GROUP):
-                if p < len(GROUPS) and r < GROUPS[p] and scaled_on_gpsimd(p, r):
-                    copy_factor(p, r)
-                    gpsimd_scale(p, r)
-            group_stage(one_plus, p + 1)
-            tile_stage(sums, p + 2, 0)
-            for r in range(MAX_GROUP):
-                if p < len(GROUPS) and r < GROUPS[p] and not scaled_on_gpsimd(p, r):
-                    scale(p, r)
+                if 0 <= p < len(GROUPS) and r < GROUPS[p] and not scaled_on_gpsimd(p, r):
+                    tile_stage(scale, p, r)
                 tile_stage(squares, p + 3, r)
                 tile_stage(transpose, p, r)
-                if r == 0:
-                    tile_stage(sums, p + 2, 2)
-                if r == 1:
-                    tile_stage(sums, p + 2, 1)
+                if r < 2:
+                    tile_stage(sums, p + 2, 1, r)
                 if r == 2:
-                    tile_stage(sums, p + 2, 3, range(HALF_CAP))
-                if r == 1:
-                    group_stage(denom, p + 1)
-                    group_stage(recip, p + 1)
+                    tile_stage(sums, p + 2, 2)
+                if r == 2:
+                    group_stage(one_plus, p + 2)
                 tile_stage(evacuate, p, r)
             group_stage(factor, p + 1)
-            tile_stage(sums, p + 2, 3, range(HALF_CAP, CAP_LEN))
+            if p == WPREP:
+                quantise_weights()
+                widen_bias()
+            tile_stage(sums, p + 3, 0)
+            group_stage(finish, p - 2)
             group_stage(quantise, p - 1)
             group_stage(multiply, p - 1)
-            group_stage(finish, p - 2)
+            group_stage(denom, p + 2)
+            if p >= HOLD_FROM:
+                group_stage(hold_gpsimd, p + 2)
 
         with tc.manual_schedule():
             ident = const.tile([P, P], F32)
@@ -300,28 +321,36 @@ def tile_capsulenetwork_pc_t_kernel(tc, s, Wc, bc, out):
             w_grouped = const.tile([P, PASSES, N_OUT, 2 * HALVES], BF16, align_bytes=64)
             w_codes = const.tile([P, PASSES, N_OUT], U32, align_bytes=64)
             w_scales = const.tile([P, PASSES, N_OUT], U8, align_bytes=64)
-            load(0)
-            load(1)
-            load(2)
+            for g in range(4):
+                load(g)
             load_weights()
             load_bias()
-            for g in range(3, 3 + LOADS_AHEAD):
+            for g in range(4, 3 + LOADS_AHEAD):
                 load(g)
-            squares(0, 0)
-            squares(0, 1)
-            squares(1, 0)
-            squares(1, 1)
-            sums(0, 0)
-            sums(0, 1)
-            one_plus(0)
-            denom(0)
-            recip(0)
-            sums(1, 0)
-            sums(1, 1)
-            factor(0)
-            for r in range(GROUPS[2]):
-                squares(2, r)
-            quantise_weights()
-            widen_bias()
+            tile_stage(squares, 0, 0)
+            tile_stage(squares, 0, 1)
+            tile_stage(squares, 1, 0)
+            tile_stage(squares, 1, 1)
+            all_tiles(sums, 0)
+            group_stage(one_plus, 0)
+            group_stage(denom, 0)
+            group_stage(recip, 0)
+            tile_stage(squares, 2, 1)
+            all_tiles(sums, 1)
+            group_stage(factor, 0)
+            tile_stage(squares, 2, 0)
+            tile_stage(squares, 2, 3)
+            tile_stage(squares, 2, 2)
+            tile_stage(sums, 2, 1)
+            tile_stage(sums, 2, 0)
+            tile_stage(sums, 2, 3)
+            group_stage(one_plus, 1)
+            tile_stage(scale, 0, 0)
+            group_stage(denom, 1)
+            group_stage(recip, 1)
+            tile_stage(sums, 2, 2)
+            group_stage(one_plus, 2)
+            all_tiles(squares, 3)
+            tile_stage(transpose, 0, 0)
             for p in range(len(GROUPS) + 2):
                 period(p)

@@ -33,6 +33,7 @@ GPSIMD_HEAD_SQUARES = ()
 E_PERIOD = 1000
 E_TAIL = 2
 HOLD_FROM = 1
+GSQ = [(1, 3), (1,)]
 WPREP = 1
 SCALAR_SQUARES = ()
 LOADS_AHEAD = 3
@@ -86,7 +87,7 @@ def tile_capsulenetwork_pc_t_kernel(tc, s, Wc, bc, out):
 
         def on_gpsimd(g, r):
             t = FIRST[g] + r
-            return t in GPSIMD_HEAD_SQUARES or GROUPS[g] == MAX_GROUP and r % 2 == 1 and t not in VECTOR_SQUARES + SCALAR_SQUARES
+            return t in GPSIMD_HEAD_SQUARES or GROUPS[g] == MAX_GROUP and r in GSQ[g % len(GSQ)] and t not in VECTOR_SQUARES + SCALAR_SQUARES
 
         def scaled_on_gpsimd(g, r):
             if g < 3 or GROUPS[g] < MAX_GROUP:
@@ -97,9 +98,7 @@ def tile_capsulenetwork_pc_t_kernel(tc, s, Wc, bc, out):
             x = x_of[g][:, r]
             if on_gpsimd(g, r):
                 sq = sq_pool.tile([P, CAPS, CAP_LEN], F32)
-                for first in range(0, CAPS, CAPS // 2):
-                    part = slice(first, first + CAPS // 2)
-                    nc.gpsimd.tensor_tensor(out=sq[:, part], in0=x[:, part], in1=x[:, part], op=ALU.mult)
+                nc.gpsimd.tensor_tensor(out=sq[:], in0=x, in1=x, op=ALU.mult)
                 planes_of[g, r] = [sq[:, :, o] for o in range(CAP_LEN)]
             else:
                 sq_planes = sq_pool.tile([P, CAP_LEN, CAPS], F32)
@@ -172,13 +171,12 @@ def tile_capsulenetwork_pc_t_kernel(tc, s, Wc, bc, out):
 
         def gpsimd_scale(g, r):
             v = v_pool.tile([P, HALVES, CAPS, HALF_CAP], BF16)
-            for u in range(HALVES):
-                nc.gpsimd.tensor_tensor(
-                    out=v[:, u],
-                    in0=x_of[g][:, r, :, u * HALF_CAP : (u + 1) * HALF_CAP],
-                    in1=fsb_of[g, r][:].unsqueeze(2).to_broadcast([P, CAPS, HALF_CAP]),
-                    op=ALU.mult,
-                )
+            nc.gpsimd.tensor_tensor(
+                out=v[:],
+                in0=x_of[g][:, r].rearrange("p j (u d) -> p u j d", u=HALVES),
+                in1=fsb_of[g, r][:].unsqueeze(1).unsqueeze(3).to_broadcast([P, HALVES, CAPS, HALF_CAP]),
+                op=ALU.mult,
+            )
             v_of[g, r] = v
 
         def transpose(g, r):

@@ -33,7 +33,8 @@ GPSIMD_HEAD_SQUARES = ()
 E_PERIOD = 1000
 E_TAIL = 2
 HOLD_FROM = 1
-GSQ = [(1, 3), (1,)]
+GSQ = [(1, 3)]
+GCUT = 80
 WPREP = 1
 SCALAR_SQUARES = ()
 LOADS_AHEAD = 3
@@ -46,7 +47,8 @@ def tile_capsulenetwork_pc_t_kernel(tc, s, Wc, bc, out):
     with ExitStack() as ctx:
         const = ctx.enter_context(tc.tile_pool(name="const", bufs=1))
         x_pool = ctx.enter_context(tc.tile_pool(name="x", bufs=7))
-        sq_pool = ctx.enter_context(tc.tile_pool(name="sq", bufs=10))
+        sq_pool = ctx.enter_context(tc.tile_pool(name="sq", bufs=8))
+        sq2_pool = ctx.enter_context(tc.tile_pool(name="sq2", bufs=3))
         small = ctx.enter_context(tc.tile_pool(name="small", bufs=3))
         v_pool = ctx.enter_context(tc.tile_pool(name="v", bufs=4))
         mx_pool = ctx.enter_context(tc.tile_pool(name="mx", bufs=3))
@@ -58,6 +60,7 @@ def tile_capsulenetwork_pc_t_kernel(tc, s, Wc, bc, out):
 
         x_of = {}
         planes_of = {}
+        pair_of = {}
         fsb_of = {}
         q_of = {}
         one_plus_of = {}
@@ -94,22 +97,45 @@ def tile_capsulenetwork_pc_t_kernel(tc, s, Wc, bc, out):
                 return False
             return r == 3 and g >= len(GROUPS) - len(TAIL) - E_TAIL
 
-        def squares(g, r):
+        def squares_gpsimd(g, r):
             x = x_of[g][:, r]
+            sq = sq_pool.tile([P, CAPS, CAP_LEN], F32)
+            cut = CAPS if r == 1 else GCUT
+            nc.gpsimd.tensor_tensor(out=sq[:, :cut], in0=x[:, :cut], in1=x[:, :cut], op=ALU.mult)
+            if cut < CAPS:
+                nc.scalar.activation(out=sq[:, cut:], in_=x[:, cut:], func=ACT.Square)
+            planes_of[g, r] = [sq[:, :, o] for o in range(CAP_LEN)]
+
+        def squares_planes(g, r):
+            x = x_of[g][:, r]
+            sq_planes = sq_pool.tile([P, CAP_LEN, CAPS], F32)
+            for first in range(0, CAP_LEN, HALF_CAP):
+                part = slice(first, first + HALF_CAP)
+                out_part = sq_planes[:, part].rearrange("p o j -> p j o")
+                if FIRST[g] + r in VECTOR_SQUARES:
+                    nc.vector.tensor_tensor(out=out_part, in0=x[:, :, part], in1=x[:, :, part], op=ALU.mult)
+                else:
+                    nc.scalar.activation(out=out_part, in_=x[:, :, part], func=ACT.Square)
+            planes_of[g, r] = [sq_planes[:, o, :] for o in range(CAP_LEN)]
+
+        def squares(g, r):
             if on_gpsimd(g, r):
-                sq = sq_pool.tile([P, CAPS, CAP_LEN], F32)
-                nc.gpsimd.tensor_tensor(out=sq[:], in0=x, in1=x, op=ALU.mult)
-                planes_of[g, r] = [sq[:, :, o] for o in range(CAP_LEN)]
+                squares_gpsimd(g, r)
             else:
-                sq_planes = sq_pool.tile([P, CAP_LEN, CAPS], F32)
-                for first in range(0, CAP_LEN, HALF_CAP):
-                    part = slice(first, first + HALF_CAP)
-                    out_part = sq_planes[:, part].rearrange("p o j -> p j o")
-                    if FIRST[g] + r in VECTOR_SQUARES:
-                        nc.vector.tensor_tensor(out=out_part, in0=x[:, :, part], in1=x[:, :, part], op=ALU.mult)
-                    else:
-                        nc.scalar.activation(out=out_part, in_=x[:, :, part], func=ACT.Square)
-                planes_of[g, r] = [sq_planes[:, o, :] for o in range(CAP_LEN)]
+                squares_planes(g, r)
+
+        def squares_pair(g, half):
+            if half == 0:
+                pair = sq2_pool.tile([P, 2, CAP_LEN, CAPS], F32)
+                for i in range(2):
+                    planes_of[g, 2 * i] = [pair[:, i, o, :] for o in range(CAP_LEN)]
+                pair_of[g] = pair
+            part = slice(half * HALF_CAP, (half + 1) * HALF_CAP)
+            nc.scalar.activation(
+                out=pair_of[g][:, :, part].rearrange("p r o j -> p r j o"),
+                in_=x_of[g][:, 0:3:2, :, part],
+                func=ACT.Square,
+            )
 
         def sums(g, r, half=None):
             if g not in q_of:
@@ -285,7 +311,10 @@ def tile_capsulenetwork_pc_t_kernel(tc, s, Wc, bc, out):
             for r in range(MAX_GROUP):
                 if 0 <= p < len(GROUPS) and r < GROUPS[p] and not scaled_on_gpsimd(p, r):
                     tile_stage(scale, p, r)
-                tile_stage(squares, p + 3, r)
+                if 3 < p + 3 < len(GROUPS) and GROUPS[p + 3] == MAX_GROUP and r in (0, 2):
+                    squares_pair(p + 3, r // 2)
+                else:
+                    tile_stage(squares, p + 3, r)
                 tile_stage(transpose, p, r)
                 if r < 2:
                     tile_stage(sums, p + 2, 1, r)

from contextlib import ExitStack

import concourse.mybir as mybir
from concourse.masks import make_identity

F32 = mybir.dt.float32
BF16 = mybir.dt.bfloat16
U32 = mybir.dt.uint32
U8 = mybir.dt.uint8
FP8X4 = mybir.dt.float8_e4m3fn_x4
ALU = mybir.AluOpType
ACT = mybir.ActivationFunctionType

P = 128
ROWS = 8192
CAPS = 128
CAP_LEN = 8
HALF_CAP = CAP_LEN // 2
K = CAPS * CAP_LEN
N_OUT = 128
SQ_EPS = 1e-8
TILES = ROWS // P
PASSES = K // (4 * P)
HALVES = 2

HEAD = [2, 2]
TAIL = [2, 2]
MAX_GROUP = 4
GROUPS = HEAD + [MAX_GROUP] * ((TILES - sum(HEAD) - sum(TAIL)) // MAX_GROUP) + TAIL
FIRST = [sum(GROUPS[:g]) for g in range(len(GROUPS))]
VECTOR_SQUARES = (1, 3, 5, 7, 9)
GPSIMD_HEAD_SQUARES = ()
E_PERIOD = 1000
E_TAIL = 2
HOLD_FROM = 1
GSQ = [(1, 3)]
GCUT = 80
WPREP = 1
SCALAR_SQUARES = ()
LOADS_AHEAD = 3

FLOPS = 2 * ROWS * K * N_OUT


def tile_capsulenetwork_pc_t_kernel(tc, s, Wc, bc, out):
    nc = tc.nc
    with ExitStack() as ctx:
        const = ctx.enter_context(tc.tile_pool(name="const", bufs=1))
        x_pool = ctx.enter_context(tc.tile_pool(name="x", bufs=7))
        sq_pool = ctx.enter_context(tc.tile_pool(name="sq", bufs=8))
        sq2_pool = ctx.enter_context(tc.tile_pool(name="sq2", bufs=3))
        small = ctx.enter_context(tc.tile_pool(name="small", bufs=3))
        v_pool = ctx.enter_context(tc.tile_pool(name="v", bufs=4))
        mx_pool = ctx.enter_context(tc.tile_pool(name="mx", bufs=3))
        res_pool = ctx.enter_context(tc.tile_pool(name="res", bufs=2))
        q_psum = ctx.enter_context(tc.psum_pool(name="q_psum", bufs=2))
        f_psum = ctx.enter_context(tc.psum_pool(name="f_psum", bufs=1))
        t_psum = ctx.enter_context(tc.psum_pool(name="t_psum", bufs=4))
        o_psum = ctx.enter_context(tc.psum_pool(name="o_psum", bufs=1))

        x_of = {}
        planes_of = {}
        pair_of = {}
        fsb_of = {}
        q_of = {}
        one_plus_of = {}
        denom_of = {}
        recip_of = {}
        f_of = {}
        v_of = {}
        vt_of = {}
        grouped_of = {}
        codes_of = {}
        scales_of = {}
        acc_of = {}
        acc_sb_of = {}

        def rows_of(g):
            return slice(FIRST[g] * P, (FIRST[g] + GROUPS[g]) * P)

        def load(g):
            x = x_pool.tile([P, GROUPS[g], CAPS, CAP_LEN], BF16)
            rows = s[rows_of(g)].rearrange("(p r) j o -> p r (j o)", r=GROUPS[g])
            step = 1 if g < 2 else 2 if g == 2 else GROUPS[g]
            for r in range(0, GROUPS[g], step):
                nc.sync.dma_start(
                    out=x[:, r : r + step].rearrange("p r j o -> p r (j o)"), in_=rows[:, r : r + step]
                )
            x_of[g] = x

        def on_gpsimd(g, r):
            t = FIRST[g] + r
            return t in GPSIMD_HEAD_SQUARES or GROUPS[g] == MAX_GROUP and r in GSQ[g % len(GSQ)] and t not in VECTOR_SQUARES + SCALAR_SQUARES

        def scaled_on_gpsimd(g, r):
            if g < 3 or GROUPS[g] < MAX_GROUP:
                return False
            return r == 3 and g >= len(GROUPS) - len(TAIL) - E_TAIL

        def squares_gpsimd(g, r):
            x = x_of[g][:, r]
            sq = sq_pool.tile([P, CAPS, CAP_LEN], F32)
            cut = CAPS if r == 1 else GCUT
            nc.gpsimd.tensor_tensor(out=sq[:, :cut], in0=x[:, :cut], in1=x[:, :cut], op=ALU.mult)
            if cut < CAPS:
                nc.scalar.activation(out=sq[:, cut:], in_=x[:, cut:], func=ACT.Square)
            planes_of[g, r] = [sq[:, :, o] for o in range(CAP_LEN)]

        def squares_planes(g, r):
            x = x_of[g][:, r]
            sq_planes = sq_pool.tile([P, CAP_LEN, CAPS], F32)
            for first in range(0, CAP_LEN, HALF_CAP):
                part = slice(first, first + HALF_CAP)
                out_part = sq_planes[:, part].rearrange("p o j -> p j o")
                if FIRST[g] + r in VECTOR_SQUARES:
                    nc.vector.tensor_tensor(out=out_part, in0=x[:, :, part], in1=x[:, :, part], op=ALU.mult)
                else:
                    nc.scalar.activation(out=out_part, in_=x[:, :, part], func=ACT.Square)
            planes_of[g, r] = [sq_planes[:, o, :] for o in range(CAP_LEN)]

        def squares(g, r):
            if on_gpsimd(g, r):
                squares_gpsimd(g, r)
            else:
                squares_planes(g, r)

        def squares_pair(g, half):
            if half == 0:
                pair = sq2_pool.tile([P, 2, CAP_LEN, CAPS], F32)
                for i in range(2):
                    planes_of[g, 2 * i] = [pair[:, i, o, :] for o in range(CAP_LEN)]
                pair_of[g] = pair
            part = slice(half * HALF_CAP, (half + 1) * HALF_CAP)
            nc.scalar.activation(
                out=pair_of[g][:, :, part].rearrange("p r o j -> p r j o"),
                in_=x_of[g][:, 0:3:2, :, part],
                func=ACT.Square,
            )

        def sums(g, r, half=None):
            if g not in q_of:
                q_t = q_psum.tile([P, MAX_GROUP, P], F32)
                q_of[g] = q_t
            for o in range(CAP_LEN) if half is None else range(half * HALF_CAP, (half + 1) * HALF_CAP):
                nc.tensor.matmul(
                    out=q_of[g][:, r, :],
                    lhsT=planes_of[g, r][o],
                    rhs=ident[:],
                    is_transpose=True,
                    start=(o == 0),
                    stop=(o == CAP_LEN - 1),
                )

        def one_plus(g):
            one_plus_sq = small.tile([P, GROUPS[g], P], F32)
            nc.scalar.activation(out=one_plus_sq[:], in_=q_of[g][:, : GROUPS[g]], func=ACT.Square, bias=one_col[:, 0:1])
            one_plus_of[g] = one_plus_sq

        def denom(g):
            denom_sq = small.tile([P, GROUPS[g], P], F32)
            nc.vector.scalar_tensor_tensor(
                out=denom_sq[:], in0=q_of[g][:, : GROUPS[g]], scalar=SQ_EPS, in1=one_plus_of[g][:], op0=ALU.add, op1=ALU.mult
            )
            denom_of[g] = denom_sq

        def hold_gpsimd(g):
            token = small.tile([P, 1], F32)
            nc.gpsimd.tensor_copy(out=token[:], in_=denom_of[g][:, 0, 0:1])

        def recip(g):
            recip_t = small.tile([P, GROUPS[g], P], F32)
            nc.scalar.activation(out=recip_t[:], in_=denom_of[g][:], func=ACT.Abs_reciprocal_sqrt)
            recip_of[g] = recip_t

        def factor(g):
            f_t = small.tile([P, GROUPS[g], P], F32)
            nc.vector.tensor_tensor(out=f_t[:], in0=recip_of[g][:], in1=q_of[g][:, : GROUPS[g]], op=ALU.mult)
            f_rows = f_psum.tile([P, MAX_GROUP, CAPS], F32)
            for r in range(GROUPS[g]):
                nc.tensor.transpose(out=f_rows[:, r, :], in_=f_t[:, r, :], identity=ident[:])
            f_of[g] = f_rows

        def scale(g, r):
            v = v_pool.tile([P, HALVES, CAPS, HALF_CAP], BF16)
            nc.vector.tensor_tensor(
                out=v[:],
                in0=x_of[g][:, r].rearrange("p j (u d) -> p u j d", u=HALVES),
                in1=f_of[g][:, r, :].unsqueeze(1).unsqueeze(3).to_broadcast([P, HALVES, CAPS, HALF_CAP]),
                op=ALU.mult,
            )
            v_of[g, r] = v

        def copy_factor(g, r):
            f_sb = small.tile([P, CAPS], F32)
            nc.scalar.copy(out=f_sb[:], in_=f_of[g][:, r, :])
            fsb_of[g, r] = f_sb

        def gpsimd_scale(g, r):
            v = v_pool.tile([P, HALVES, CAPS, HALF_CAP], BF16)
            nc.gpsimd.tensor_tensor(
                out=v[:],
                in0=x_of[g][:, r].rearrange("p j (u d) -> p u j d", u=HALVES),
                in1=fsb_of[g, r][:].unsqueeze(1).unsqueeze(3).to_broadcast([P, HALVES, CAPS, HALF_CAP]),
                op=ALU.mult,
            )
            v_of[g, r] = v

        def transpose(g, r):
            v_words = v_of[g, r][:].rearrange("p u j d -> p (u j d)").bitcast(F32)
            v_t = t_psum.tile([P, PASSES, HALVES, P], F32)
            for c in range(PASSES):
                for u in range(HALVES):
                    first = (u * PASSES + c) * P
                    nc.tensor.transpose(
                        out=v_t[:, c, u, :], in_=v_words[:, first : first + P], identity=ident[:]
                    )
            vt_of[g, r] = v_t

        def evacuate(g, r):
            if r == 0:
                grouped = mx_pool.tile([P, GROUPS[g], PASSES, P, HALVES], F32, align_bytes=64)
                grouped_of[g] = grouped
            nc.scalar.copy(out=grouped_of[g][:, r], in_=vt_of[g, r][:].rearrange("q c u p -> q c p u"))

        def quantise(g):
            codes = mx_pool.tile([P, GROUPS[g], PASSES, P], U32, align_bytes=64)
            scales = mx_pool.tile([P, GROUPS[g], PASSES, P], U8, align_bytes=64)
            nc.vector.quantize_mx(
                out=codes[:].rearrange("q r c p -> q (r c p)").bitcast(FP8X4),
                scales=scales[:].rearrange("q r c p -> q (r c p)"),
                in_=grouped_of[g][:].rearrange("q r c p u -> q (r c p u)").bitcast(BF16),
            )
            codes_of[g] = codes
            scales_of[g] = scales

        def multiply(g):
            acc = o_psum.tile([P, MAX_GROUP, N_OUT], F32)
            for r in range(GROUPS[g]):
                for c in range(PASSES):
                    nc.tensor.matmul_mx(
                        out=acc[:, r, :],
                        lhsT=codes_of[g][:, r, c, :].bitcast(FP8X4),
                        lhsT_scale=scales_of[g][:, r, c, :],
                        rhs=w_codes[:, c, :].bitcast(FP8X4),
                        rhs_scale=w_scales[:, c, :],
                        start=(c == 0),
                        stop=(c == PASSES - 1),
                    )
            acc_of[g] = acc

        def finish(g):
            res = res_pool.tile([P, GROUPS[g], N_OUT], F32)
            nc.vector.tensor_tensor(
                out=res[:],
                in0=bias[:].unsqueeze(1).to_broadcast([P, GROUPS[g], N_OUT]),
                in1=acc_of[g][:, : GROUPS[g]],
                op=ALU.add,
            )
            nc.sync.dma_start(
                out=out[rows_of(g)].rearrange("(p r) n -> p (r n)", r=GROUPS[g]),
                in_=res[:].rearrange("p r n -> p (r n)"),
            )

        def load_bias():
            nc.sync.dma_start(out=bias_bf[:], in_=bc.partition_broadcast(P))

        def load_weights():
            rows = Wc.rearrange("(c j u i e) n -> c i j u (e n)", c=PASSES, u=HALVES, i=2, e=2)
            for c in range(PASSES):
                for i in range(2):
                    nc.sync.dma_start(
                        out=w_raw[i:P:2, c].rearrange("q (u e) n -> q u (e n)", u=HALVES), in_=rows[c, i]
                    )

        def quantise_weights():
            nc.vector.tensor_copy(out=w_grouped[:], in_=w_raw[:].rearrange("q c t n -> q c n t"))
            nc.vector.quantize_mx(
                out=w_codes[:].rearrange("q c n -> q (c n)").bitcast(FP8X4),
                scales=w_scales[:].rearrange("q c n -> q (c n)"),
                in_=w_grouped[:].rearrange("q c n t -> q (c n t)"),
            )

        def widen_bias():
            nc.vector.tensor_copy(out=bias[:], in_=bias_bf[:])

        done = set()

        def group_stage(stage, g):
            if 0 <= g < len(GROUPS) and (stage, g) not in done:
                done.add((stage, g))
                stage(g)

        def tile_stage(stage, g, r, *more):
            if 0 <= g < len(GROUPS) and r < GROUPS[g] and (stage, g, r) not in done and (stage, g, r, *more) not in done:
                done.add((stage, g, r, *more))
                stage(g, r, *more)

        def all_tiles(stage, g):
            for r in range(GROUPS[g]):
                tile_stage(stage, g, r)

        def period(p):
            group_stage(load, p + 3 + LOADS_AHEAD)
            if 0 <= p < len(GROUPS):
                for r in range(GROUPS[p]):
                    if scaled_on_gpsimd(p, r):
                        copy_factor(p, r)
                        gpsimd_scale(p, r)
            group_stage(recip, p + 1)
            tile_stage(sums, p + 2, 3)
            for r in range(MAX_GROUP):
                if 0 <= p < len(GROUPS) and r < GROUPS[p] and not scaled_on_gpsimd(p, r):
                    tile_stage(scale, p, r)
                if 3 < p + 3 < len(GROUPS) and GROUPS[p + 3] == MAX_GROUP and r in (0, 2):
                    squares_pair(p + 3, r // 2)
                else:
                    tile_stage(squares, p + 3, r)
                tile_stage(transpose, p, r)
                if r < 2:
                    tile_stage(sums, p + 2, 1, r)
                if r == 2:
                    tile_stage(sums, p + 2, 2)
                if r == 2:
                    group_stage(one_plus, p + 2)
                tile_stage(evacuate, p, r)
            group_stage(factor, p + 1)
            if p == WPREP:
                quantise_weights()
                widen_bias()
            tile_stage(sums, p + 3, 0)
            group_stage(finish, p - 2)
            group_stage(quantise, p - 1)
            group_stage(multiply, p - 1)
            group_stage(denom, p + 2)
            if p >= HOLD_FROM:
                group_stage(hold_gpsimd, p + 2)

        with tc.manual_schedule():
            ident = const.tile([P, P], F32)
            make_identity(nc, ident[:])
            one_col = const.tile([P, 1], F32)
            nc.vector.memset(one_col[:], 1.0)
            warm = const.tile([P, 1], F32)
            nc.scalar.activation(out=warm[:], in_=one_col[:], func=ACT.Abs_reciprocal_sqrt)
            bias_bf = const.tile([P, N_OUT], BF16)
            bias = const.tile([P, N_OUT], F32)
            w_raw = const.tile([P, PASSES, 2 * HALVES, N_OUT], BF16)
            w_grouped = const.tile([P, PASSES, N_OUT, 2 * HALVES], BF16, align_bytes=64)
            w_codes = const.tile([P, PASSES, N_OUT], U32, align_bytes=64)
            w_scales = const.tile([P, PASSES, N_OUT], U8, align_bytes=64)
            for g in range(4):
                load(g)
            load_weights()
            load_bias()
            for g in range(4, 3 + LOADS_AHEAD):
                load(g)
            tile_stage(squares, 0, 0)
            tile_stage(squares, 0, 1)
            tile_stage(squares, 1, 0)
            tile_stage(squares, 1, 1)
            all_tiles(sums, 0)
            group_stage(one_plus, 0)
            group_stage(denom, 0)
            group_stage(recip, 0)
            tile_stage(squares, 2, 1)
            all_tiles(sums, 1)
            group_stage(factor, 0)
            tile_stage(squares, 2, 0)
            tile_stage(squares, 2, 3)
            tile_stage(squares, 2, 2)
            tile_stage(sums, 2, 1)
            tile_stage(sums, 2, 0)
            tile_stage(sums, 2, 3)
            group_stage(one_plus, 1)
            tile_stage(scale, 0, 0)
            group_stage(denom, 1)
            group_stage(recip, 1)
            tile_stage(sums, 2, 2)
            group_stage(one_plus, 2)
            all_tiles(squares, 3)
            tile_stage(transpose, 0, 0)
            for p in range(len(GROUPS) + 2):
                period(p)
